import numpy as np
import ml_dtypes


def mxq(x, axis, fmt="e4m3"):
    dtype, down = {"e4m3": (ml_dtypes.float8_e4m3fn, 7), "e5m2": (ml_dtypes.float8_e5m2, 14)}[fmt]
    v = np.moveaxis(np.asarray(x, np.float32).astype(ml_dtypes.bfloat16).astype(np.float64), axis, -1)
    blocks = v.reshape(v.shape[:-1] + (-1, 32))
    amax = np.abs(blocks).max(-1, keepdims=True)
    byte = np.maximum(np.where(amax > 0, np.frexp(amax)[1] - 1 + 127, 0) - down, 1)
    scale = np.exp2(byte - 127.0)
    codes = (blocks / scale).astype(np.float32).astype(dtype).astype(np.float64)
    return np.moveaxis((codes * scale).reshape(v.shape), -1, axis)


WIDE = False


def mx_kscale(k):
    if not WIDE:
        return np.ones(k)
    levels = np.array([10, -10, 5, -5, 0])
    if k % 512:
        return np.exp2(np.random.permutation(np.resize(levels, k // 32))).repeat(32)
    a = np.empty((k // 512, 16))
    for p in range(k // 512):
        a[p, :8] = np.random.permutation(np.resize(levels, 8))
        for g in range(8):
            far = levels[np.abs(levels - a[p, g]) >= 10]
            a[p, g + 8] = far[np.random.randint(len(far))]
    return np.exp2(a.ravel()).repeat(32)


BF16 = ml_dtypes.bfloat16


def bf(x):
    return np.asarray(x, np.float32).astype(BF16)


def f64(x):
    return np.asarray(x).astype(np.float64)


B, K, H, D = 2048, 512, 512, 2
C = 0.2
HALF_LOG_2PI = 0.5 * np.log(2.0 * np.pi)


def log_softmax(v, axis):
    v = v - v.max(axis=axis, keepdims=True)
    return v - np.log(np.exp(v).sum(axis=axis, keepdims=True))


def logsumexp(v, axis):
    m = v.max(axis=axis, keepdims=True)
    return np.log(np.exp(v - m).sum(axis=axis)) + np.squeeze(m, axis)


def contract(xq, vq):
    return (xq.transpose(2, 0, 1) @ vq.transpose(2, 1, 0)).transpose(1, 2, 0)


def setup_inputs():
    s = mx_kscale(H)[None, :, None]
    r = 1.0 / np.sqrt(H)
    return {
        "x": bf(np.random.standard_normal((B, H, D)) * s),
        "input_var": bf(np.random.standard_normal((B, D)) * C),
        "V_alpha": bf(np.random.standard_normal((K, H, D)) * r / s),
        "V_mu": bf(np.random.standard_normal((K, H, D)) * C * r / s),
        "V_sigma": bf(np.random.standard_normal((K, H, D)) * 0.5 * r / s),
        "b_alpha": bf(np.random.standard_normal((K, D)) * 0.7),
        "b_mu": bf(np.random.standard_normal((K, D)) * 0.5 * C),
        "b_sigma": bf(np.log(C) + np.random.standard_normal((K, D)) * 0.3),
    }


def reference(x, input_var, V_alpha, V_mu, V_sigma, b_alpha, b_mu, b_sigma):
    xq = mxq(f64(x), 1, "e4m3")
    exp_alpha = contract(xq, mxq(f64(V_alpha), 1, "e4m3")) + f64(b_alpha)
    log_alpha = log_softmax(exp_alpha, 1)
    mu = contract(xq, mxq(f64(V_mu), 1, "e4m3")) + f64(b_mu)
    log_sigma = np.clip(contract(xq, mxq(f64(V_sigma), 1, "e4m3")) + f64(b_sigma), -20.0, 20.0)
    sigma = np.exp(log_sigma)
    y = f64(input_var)[:, None, :]
    log_p = -0.5 * np.square((y - mu) / sigma) + log_alpha - HALF_LOG_2PI - log_sigma
    return np.sum(logsumexp(log_p, 1), axis=1)

@@ -1,0 +1,480 @@
+import math
+from contextlib import ExitStack
+
+import concourse.mybir as mybir
+from concourse.masks import make_identity
+
+F32 = mybir.dt.float32
+BF16 = mybir.dt.bfloat16
+U32 = mybir.dt.uint32
+I32 = mybir.dt.int32
+U8 = mybir.dt.uint8
+FP8X4 = mybir.dt.float8_e4m3fn_x4
+ALU = mybir.AluOpType
+ACT = mybir.ActivationFunctionType
+AXIS = mybir.AxisListType
+
+P = 128
+PACK = 4
+B, K, H, D = 2048, 512, 512, 2
+H_HIGH = H // PACK
+N_COLS = 512
+BANK_BF16 = 1024
+X_ROWS = BANK_BF16 // (PACK * P)
+KT = K // P
+N_CHUNKS = B // N_COLS
+BLOCKS = N_COLS // P
+STEPS = N_CHUNKS * D * KT
+X_BANKS = 2 * D
+LAG_T = KT + 3
+LAG_A = KT + 1
+CLIP = 20.0
+SIGMA, MU, ALPHA = 0, 1, 2
+
+FLOPS = 2 * B * K * H * D * 3
+
+
+def tile_rnadeoutputlayer_t_kernel(
+    tc, x, input_var, V_alpha, V_mu, V_sigma, b_alpha, b_mu, b_sigma, out
+):
+    nc = tc.nc
+    weights = (V_sigma, V_mu, V_alpha)
+    biases = (b_sigma, b_mu, b_alpha)
+
+    with ExitStack() as ctx:
+        const = ctx.enter_context(tc.tile_pool(name="const", bufs=1))
+        raw = ctx.enter_context(tc.tile_pool(name="raw", bufs=1))
+        stage = ctx.enter_context(tc.tile_pool(name="stage", bufs=3))
+        work = ctx.enter_context(tc.tile_pool(name="work", bufs=4))
+        keep = ctx.enter_context(tc.tile_pool(name="keep", bufs=3 * KT))
+        mx_psum = ctx.enter_context(tc.psum_pool(name="mx_psum", bufs=1))
+        tp_psum = ctx.enter_context(tc.psum_pool(name="tp_psum", bufs=4))
+        ctx.enter_context(tc.manual_schedule())
+
+        x_rows = x.rearrange("(r p) h d -> p r (h d)", p=P)
+        x_tiles_per_chunk = N_COLS // P
+
+        def load_x(chunk):
+            x_raw = raw.tile([P, x_tiles_per_chunk, H_HIGH, PACK, D], BF16, name="x_raw%d" % chunk)
+            half = x_tiles_per_chunk // 2
+            for part in range(2):
+                first = chunk * x_tiles_per_chunk + part * half
+                nc.sync.dma_start(
+                    out=x_raw[:, part * half : (part + 1) * half].rearrange("p r hp t d -> p r (hp t d)"),
+                    in_=x_rows[:, first : first + half, :],
+                )
+            return x_raw
+
+        def load_weight(w, kt):
+            v_raw = raw.tile([P, H_HIGH, PACK, D], BF16, name="v_raw%d_%d" % (w, kt))
+            nc.sync.dma_start(
+                out=v_raw[:].rearrange("p hp t d -> p (hp t d)"),
+                in_=weights[w][kt * P : (kt + 1) * P].rearrange("k h d -> k (h d)"),
+            )
+            return v_raw
+
+        v_raws = {}
+        x_raws = {}
+        x_raws[0] = load_x(0)
+        for kt in range(KT):
+            for w in (SIGMA, MU, ALPHA):
+                v_raws[(w, kt)] = load_weight(w, kt)
+        for chunk in range(1, N_CHUNKS):
+            x_raws[chunk] = load_x(chunk)
+
+        bias_rows = const.tile([P, P, D], BF16)
+        nc.vector.memset(bias_rows[:], 0.0)
+        for w in (SIGMA, MU, ALPHA):
+            nc.scalar.dma_start(
+                out=bias_rows[KT * w : KT * (w + 1)].rearrange("kt kl d -> kt (kl d)"),
+                in_=biases[w].rearrange("(kt kl) d -> kt (kl d)", kt=KT),
+            )
+        y_row = const.tile([P, B * D], BF16)
+        nc.vector.memset(y_row[:].bitcast(I32), 0)
+        nc.scalar.dma_start(out=y_row[0:1, :], in_=input_var.rearrange("(o b) d -> o (b d)", o=1))
+
+        ident_bf16 = const.tile([P, P], BF16)
+        make_identity(nc, ident_bf16[:])
+        ident_f32 = const.tile([P, P], F32)
+        make_identity(nc, ident_f32[:])
+
+        ones = const.tile([P, P], BF16)
+        nc.vector.memset(ones[:], 1.0)
+
+        warm = const.tile([P, 2], F32)
+        nc.vector.memset(warm[:], 0.0)
+        nc.scalar.activation(out=warm[:, 1:2], in_=warm[:, 0:1], func=ACT.Exp)
+
+        result = const.tile([P, P], F32)
+        nc.vector.memset(result[:], 0.0)
+
+        bias = const.tile([P, D, 3 * KT], F32)
+        neg_b_sig = const.tile([P, D, KT], F32)
+        clip_low = const.tile([P, D, KT], F32)
+        clip_high = const.tile([P, D, KT], F32)
+        b_alp_sig = const.tile([P, D, KT], F32)
+        bias_banks = {}
+
+        def transpose_biases():
+            bias_banks[0] = tp_psum.tile([P, D, P], BF16, name="bias_bank", tag="bank")
+            for d in range(D):
+                nc.tensor.transpose(
+                    out=bias_banks[0][:, d, :], in_=bias_rows[:, :, d], identity=ident_bf16[:]
+                )
+
+        def bias_columns():
+            nc.vector.tensor_copy(out=bias[:], in_=bias_banks[0][:, :, 0 : 3 * KT])
+            b_sig = bias[:, :, KT * SIGMA : KT * (SIGMA + 1)]
+            b_alp = bias[:, :, KT * ALPHA : KT * (ALPHA + 1)]
+            nc.vector.tensor_scalar(
+                out=neg_b_sig[:], in0=b_sig, scalar1=-1.0, scalar2=None, op0=ALU.mult
+            )
+            nc.vector.tensor_scalar(
+                out=clip_low[:], in0=b_sig, scalar1=-1.0, scalar2=-CLIP, op0=ALU.mult, op1=ALU.add
+            )
+            nc.vector.tensor_scalar(
+                out=clip_high[:], in0=b_sig, scalar1=-1.0, scalar2=CLIP, op0=ALU.mult, op1=ALU.add
+            )
+            nc.vector.tensor_tensor(out=b_alp_sig[:], in0=b_alp, in1=b_sig, op=ALU.subtract)
+
+        n_blocks = B // P
+        neg_max = const.tile([P, 2, D, n_blocks], F32)
+        exp_sum = const.tile([P, 2, D, n_blocks], F32)
+
+        v_codes = [
+            const.tile([P, KT, D, P], U32, name="v_codes%d" % w, align_bytes=64) for w in range(3)
+        ]
+        v_scales = [
+            const.tile([P, KT, D, P], U8, name="v_scales%d" % w, align_bytes=64) for w in range(3)
+        ]
+
+        def empty_bank(n, grouped_part, bank):
+            if n % 2 == 0:
+                nc.vector.tensor_copy(out=grouped_part, in_=bank)
+            else:
+                nc.scalar.copy(out=grouped_part, in_=bank)
+
+        y_banks = {}
+        y_all = [const.tile([P, D, N_COLS], BF16, name="y_all%d" % chunk) for chunk in range(N_CHUNKS)]
+
+        def spread_y(chunk):
+            for half in range(2):
+                first = (2 * chunk + half) * N_COLS
+                y_banks[(chunk, half)] = tp_psum.tile([P, N_COLS], F32, name="y_bank", tag="bank")
+                nc.tensor.matmul(
+                    out=y_banks[(chunk, half)][:],
+                    lhsT=ones[:],
+                    rhs=y_row[:, first : first + N_COLS],
+                    start=True,
+                    stop=True,
+                )
+
+        def keep_y(chunk):
+            samples = N_COLS // D
+            for half in range(2):
+                empty_bank(
+                    half,
+                    y_all[chunk][:, :, half * samples : (half + 1) * samples],
+                    y_banks[(chunk, half)][:].rearrange("p (b d) -> p d b", d=D),
+                )
+
+        v_banks = {}
+        x_banks = {}
+
+        def transpose_weight(w, kt):
+            bank = tp_psum.tile([P, D, PACK, P], BF16, tag="bank")
+            for d in range(D):
+                for t in range(PACK):
+                    nc.tensor.transpose(
+                        out=bank[:, d, t, :], in_=v_raws[(w, kt)][:, :, t, d], identity=ident_bf16[:]
+                    )
+            v_banks[(w, kt)] = bank
+
+        def quantise_weight(w, kt):
+            v_grouped = stage.tile([P, D, P, PACK], BF16, align_bytes=64)
+            empty_bank(w, v_grouped[:], v_banks[(w, kt)][:].rearrange("p d t k -> p d k t"))
+            nc.vector.quantize_mx(
+                out=v_codes[w][:, kt].rearrange("p d k -> p (d k)").bitcast(FP8X4),
+                scales=v_scales[w][:, kt].rearrange("p d k -> p (d k)"),
+                in_=v_grouped[:].rearrange("p d k t -> p (d k t)"),
+            )
+
+        x_grouped = {}
+        x_codes = {}
+        x_scales = {}
+
+        def x_bank_place(n):
+            return n // X_BANKS, (n % X_BANKS) // 2, n % 2
+
+        def transpose_x_bank(n):
+            chunk, d, half = x_bank_place(n)
+            bank = tp_psum.tile([P, X_ROWS, PACK, P], BF16, tag="bank")
+            for r in range(X_ROWS):
+                for t in range(PACK):
+                    nc.tensor.transpose(
+                        out=bank[:, r, t, :],
+                        in_=x_raws[chunk][:, half * X_ROWS + r, :, t, d],
+                        identity=ident_bf16[:],
+                    )
+            x_banks[n] = bank
+
+        def empty_x_bank(n):
+            chunk, d, half = x_bank_place(n)
+            if half == 0:
+                x_grouped[(chunk, d)] = stage.tile(
+                    [P, 2, X_ROWS, P, PACK], BF16, name="x_grouped", align_bytes=64
+                )
+            empty_bank(n, x_grouped[(chunk, d)][:, half], x_banks[n][:].rearrange("p r t b -> p r b t"))
+
+        def quantise_x(g):
+            group = (g // D, g % D)
+            x_codes[group] = stage.tile([P, N_COLS], U32, name="x_codes", align_bytes=64)
+            x_scales[group] = stage.tile([P, N_COLS], U8, name="x_scales", align_bytes=64)
+            nc.vector.quantize_mx(
+                out=x_codes[group][:].bitcast(FP8X4),
+                scales=x_scales[group][:],
+                in_=x_grouped[group][:].rearrange("p h r b t -> p (h r b t)"),
+            )
+
+        acc = {}
+        clipped = {}
+        inv_sigma = {}
+        distance = {}
+        z = {}
+        half_z2 = {}
+        penalty = {}
+        kept = {}
+        turned = {}
+
+        def place(step):
+            return step // (D * KT), (step // KT) % D, step % KT
+
+        def product(w, step, use=""):
+            chunk, d, kt = place(step)
+            acc[(w, step, use)] = mx_psum.tile([P, N_COLS], F32, name="acc%d%s" % (w, use))
+            nc.tensor.matmul_mx(
+                out=acc[(w, step, use)][:],
+                lhsT=v_codes[w][:, kt, d, :].bitcast(FP8X4),
+                lhsT_scale=v_scales[w][:, kt, d, :],
+                rhs=x_codes[(chunk, d)][:].bitcast(FP8X4),
+                rhs_scale=x_scales[(chunk, d)][:],
+                start=True,
+                stop=True,
+            )
+
+        def clip_log_sigma(step):
+            chunk, d, kt = place(step)
+            clipped[step] = work.tile([P, N_COLS], F32, name="clipped")
+            nc.vector.tensor_scalar(
+                out=clipped[step][:],
+                in0=acc[(SIGMA, step, "")][:],
+                scalar1=clip_low[:, d, kt : kt + 1],
+                scalar2=clip_high[:, d, kt : kt + 1],
+                op0=ALU.max,
+                op1=ALU.min,
+            )
+
+        def exp_minus_log_sigma(step):
+            chunk, d, kt = place(step)
+            inv_sigma[step] = work.tile([P, N_COLS], F32, name="inv_sigma")
+            nc.scalar.activation(
+                out=inv_sigma[step][:],
+                in_=clipped[step][:],
+                func=ACT.Exp,
+                bias=neg_b_sig[:, d, kt : kt + 1],
+                scale=-1.0,
+            )
+
+        def mu_minus_y(step):
+            chunk, d, kt = place(step)
+            distance[step] = work.tile([P, N_COLS], F32, name="distance")
+            nc.vector.scalar_tensor_tensor(
+                out=distance[step][:],
+                in0=acc[(MU, step, "")][:],
+                scalar=bias[:, d, KT * MU + kt : KT * MU + kt + 1],
+                in1=y_all[chunk][:, d, :],
+                op0=ALU.add,
+                op1=ALU.subtract,
+            )
+
+        def divide_by_sigma(step):
+            z[step] = work.tile([P, N_COLS], F32, name="z")
+            nc.gpsimd.tensor_tensor(
+                out=z[step][:], in0=distance[step][:], in1=inv_sigma[step][:], op=ALU.mult
+            )
+
+        def square(step):
+            half_z2[step] = work.tile([P, N_COLS], F32, name="half_z2")
+            nc.scalar.activation(
+                out=half_z2[step][:], in_=z[step][:], func=ACT.Square, scale=math.sqrt(0.5)
+            )
+
+        def add_penalty(step):
+            penalty[step] = work.tile([P, N_COLS], F32, name="penalty")
+            nc.gpsimd.tensor_tensor(
+                out=penalty[step][:], in0=clipped[step][:], in1=half_z2[step][:], op=ALU.add
+            )
+
+        def make_a(step):
+            chunk, d, kt = place(step)
+            kept[(1, step)] = keep.tile([P, N_COLS], F32, name="a_tile")
+            nc.scalar.activation(
+                out=kept[(1, step)][:],
+                in_=acc[(ALPHA, step, "a")][:],
+                func=ACT.Identity,
+                bias=bias[:, d, KT * ALPHA + kt : KT * ALPHA + kt + 1],
+                scale=1.0,
+            )
+
+        def make_t(step):
+            chunk, d, kt = place(step)
+            kept[(0, step)] = keep.tile([P, N_COLS], F32, name="t_tile")
+            nc.vector.scalar_tensor_tensor(
+                out=kept[(0, step)][:],
+                in0=acc[(ALPHA, step, "t")][:],
+                scalar=b_alp_sig[:, d, kt : kt + 1],
+                in1=penalty[step][:],
+                op0=ALU.add,
+                op1=ALU.subtract,
+            )
+
+        def statistic(tile_, kind, block):
+            chunk, d, j = block // (D * BLOCKS), (block // BLOCKS) % D, block % BLOCKS
+            column = chunk * BLOCKS + j
+            return tile_[:, kind, d, column : column + 1]
+
+        def turn(kind, block):
+            first_step = (block // BLOCKS) * KT
+            j = block % BLOCKS
+            turned[(kind, block)] = tp_psum.tile([P, K], F32, name="turned", tag="bank")
+            for kt in range(KT):
+                nc.tensor.transpose(
+                    out=turned[(kind, block)][:, kt * P : (kt + 1) * P],
+                    in_=kept[(kind, first_step + kt)][:, j * P : (j + 1) * P],
+                    identity=ident_f32[:],
+                )
+
+        def maximum(kind, block):
+            nc.vector.tensor_reduce(
+                out=statistic(neg_max, kind, block),
+                in_=turned[(kind, block)][:],
+                axis=AXIS.X,
+                op=ALU.max,
+                negate=True,
+            )
+
+        def sum_of_exp(kind, block):
+            unread = work.tile([P, K], F32)
+            nc.scalar.activation(
+                out=unread[:],
+                in_=turned[(kind, block)][:],
+                func=ACT.Exp,
+                bias=statistic(neg_max, kind, block),
+                scale=1.0,
+                accum_out=statistic(exp_sum, kind, block),
+            )
+
+        n_x_banks = N_CHUNKS * X_BANKS
+
+        def is_step(step):
+            return 0 <= step < STEPS
+
+        def is_block(block):
+            return 0 <= block < STEPS
+
+        transpose_x_bank(0)
+        transpose_x_bank(1)
+        transpose_weight(SIGMA, 0)
+        transpose_biases()
+        empty_x_bank(0)
+        empty_x_bank(1)
+        quantise_weight(SIGMA, 0)
+        quantise_x(0)
+        bias_columns()
+        transpose_weight(MU, 0)
+        spread_y(0)
+        quantise_weight(MU, 0)
+        keep_y(0)
+        product(SIGMA, 0)
+        product(MU, 0)
+        transpose_weight(ALPHA, 0)
+        quantise_weight(ALPHA, 0)
+        for w in (SIGMA, MU, ALPHA):
+            transpose_weight(w, 1)
+        transpose_x_bank(2)
+
+        for i in range(STEPS + LAG_T + 2):
+            if is_block(i - LAG_T):
+                turn(0, i - LAG_T)
+            if is_block(i - LAG_A):
+                turn(1, i - LAG_A)
+            if is_step(i - 2):
+                square(i - 2)
+            if is_step(i - 1):
+                make_a(i - 1)
+            if is_step(i):
+                clip_log_sigma(i)
+                mu_minus_y(i)
+
+            if i + 1 < KT:
+                for w in (SIGMA, MU, ALPHA):
+                    quantise_weight(w, i + 1)
+            if i % 2 == 0 and (i + 4) // 2 < n_x_banks:
+                empty_x_bank((i + 4) // 2)
+            if 1 <= i - 2 < N_CHUNKS:
+                keep_y(i - 2)
+
+            if is_step(i - 3):
+                make_t(i - 3)
+            if is_step(i + 1):
+                product(SIGMA, i + 1)
+                product(MU, i + 1)
+            if is_step(i):
+                product(ALPHA, i, "a")
+            if is_step(i - 2):
+                product(ALPHA, i - 2, "t")
+            if is_step(i - 1):
+                divide_by_sigma(i - 1)
+            if is_step(i - 2):
+                add_penalty(i - 2)
+
+            if is_block(i - LAG_T):
+                maximum(0, i - LAG_T)
+            if is_block(i - LAG_A):
+                maximum(1, i - LAG_A)
+            if i % 4 == 2 and 1 <= (i + 2) // 4 < N_CHUNKS * D:
+                quantise_x((i + 2) // 4)
+            if is_block(i - LAG_T - 1):
+                sum_of_exp(0, i - LAG_T - 1)
+            if is_block(i - LAG_A - 1):
+                sum_of_exp(1, i - LAG_A - 1)
+            if is_step(i):
+                exp_minus_log_sigma(i)
+
+            if i + 2 < KT:
+                for w in (SIGMA, MU, ALPHA):
+                    transpose_weight(w, i + 2)
+            if i % 2 == 1 and (i + 5) // 2 < n_x_banks:
+                transpose_x_bank((i + 5) // 2)
+            if 1 <= i - 1 < N_CHUNKS:
+                spread_y(i - 1)
+
+        log_sum = const.tile([P, 2, D, n_blocks], F32)
+        nc.scalar.activation(out=log_sum[:], in_=exp_sum[:], func=ACT.Ln)
+        lse = const.tile([P, 2, D, n_blocks], F32)
+        nc.vector.tensor_tensor(out=lse[:], in0=log_sum[:], in1=neg_max[:], op=ALU.subtract)
+        per_d = const.tile([P, D, n_blocks], F32)
+        nc.vector.tensor_tensor(out=per_d[:], in0=lse[:, 0], in1=lse[:, 1], op=ALU.subtract)
+        nc.vector.scalar_tensor_tensor(
+            out=result[:, 0:n_blocks],
+            in0=per_d[:, 0, :],
+            scalar=-math.log(2.0 * math.pi),
+            in1=per_d[:, 1, :],
+            op0=ALU.add,
+            op1=ALU.add,
+        )
+        result_bank = tp_psum.tile([P, P], F32, tag="bank")
+        nc.tensor.transpose(out=result_bank[:], in_=result[:], identity=ident_f32[:])
+        out_rows = const.tile([n_blocks, P], F32)
+        nc.scalar.copy(out=out_rows[:], in_=result_bank[0:n_blocks, :])
+        nc.sync.dma_start(out=out.rearrange("(j p) -> j p", p=P), in_=out_rows[:])

@@ -17,10 +17,12 @@ AXIS = mybir.AxisListType
 P = 128
 PACK = 4
 B, K, H, D = 2048, 512, 512, 2
-H_HIGH = H // PACK
+H_LOW = H // PACK
+ROWS = P // PACK
+RUN = 8
+BLOCKS_32 = H // 32
 N_COLS = 512
 BANK_BF16 = 1024
-X_ROWS = BANK_BF16 // (PACK * P)
 KT = K // P
 N_CHUNKS = B // N_COLS
 BLOCKS = N_COLS // P
@@ -51,26 +53,29 @@ def tile_rnadeoutputlayer_t_kernel(
         tp_psum = ctx.enter_context(tc.psum_pool(name="tp_psum", bufs=4))
         ctx.enter_context(tc.manual_schedule())
 
-        x_rows = x.rearrange("(r p) h d -> p r (h d)", p=P)
-        x_tiles_per_chunk = N_COLS // P
+        def quarter_rows(a):
+            return a.rearrange("b h d -> (b h d)").rearrange(
+                "(j q m t e) -> j t q m e", q=ROWS, m=PACK * BLOCKS_32, t=PACK, e=RUN * D
+            )
+
+        x_quarters = quarter_rows(x)
+
+        def load_rows(tile_, quarters):
+            for t in range(PACK):
+                nc.sync.dma_start(
+                    out=tile_[ROWS * t : ROWS * (t + 1)].rearrange("q r (g i) d -> q (r g) (i d)", i=RUN),
+                    in_=quarters[t],
+                )
 
         def load_x(chunk):
-            x_raw = raw.tile([P, x_tiles_per_chunk, H_HIGH, PACK, D], BF16, name="x_raw%d" % chunk)
-            half = x_tiles_per_chunk // 2
-            for part in range(2):
-                first = chunk * x_tiles_per_chunk + part * half
-                nc.sync.dma_start(
-                    out=x_raw[:, part * half : (part + 1) * half].rearrange("p r hp t d -> p r (hp t d)"),
-                    in_=x_rows[:, first : first + half, :],
-                )
+            x_raw = raw.tile([P, BLOCKS, PACK, H_LOW, D], BF16, name="x_raw%d" % chunk)
+            for j in range(BLOCKS):
+                load_rows(x_raw[:, j], x_quarters[chunk * BLOCKS + j])
             return x_raw
 
         def load_weight(w, kt):
-            v_raw = raw.tile([P, H_HIGH, PACK, D], BF16, name="v_raw%d_%d" % (w, kt))
-            nc.sync.dma_start(
-                out=v_raw[:].rearrange("p hp t d -> p (hp t d)"),
-                in_=weights[w][kt * P : (kt + 1) * P].rearrange("k h d -> k (h d)"),
-            )
+            v_raw = raw.tile([P, PACK, H_LOW, D], BF16, name="v_raw%d_%d" % (w, kt))
+            load_rows(v_raw, quarter_rows(weights[w])[kt])
             return v_raw
 
         v_raws = {}
@@ -97,6 +102,12 @@ def tile_rnadeoutputlayer_t_kernel(
         make_identity(nc, ident_bf16[:])
         ident_f32 = const.tile([P, P], F32)
         make_identity(nc, ident_f32[:])
+
+        perm = const.tile([P, P], BF16)
+        nc.vector.tensor_copy(
+            out=perm[:].rearrange("p (q t) -> p t q", t=PACK),
+            in_=ident_bf16[:].rearrange("p (t q) -> p t q", t=PACK),
+        )
 
         ones = const.tile([P, P], BF16)
         nc.vector.memset(ones[:], 1.0)
@@ -182,21 +193,21 @@ def tile_rnadeoutputlayer_t_kernel(
         x_banks = {}
 
         def transpose_weight(w, kt):
-            bank = tp_psum.tile([P, D, PACK, P], BF16, tag="bank")
+            bank = tp_psum.tile([P, D, ROWS, PACK, PACK], BF16, tag="bank")
             for d in range(D):
-                for t in range(PACK):
+                for r in range(PACK):
                     nc.tensor.transpose(
-                        out=bank[:, d, t, :], in_=v_raws[(w, kt)][:, :, t, d], identity=ident_bf16[:]
+                        out=bank[:, d, :, r, :], in_=v_raws[(w, kt)][:, r, :, d], identity=perm[:]
                     )
             v_banks[(w, kt)] = bank
 
         def quantise_weight(w, kt):
-            v_grouped = stage.tile([P, D, P, PACK], BF16, align_bytes=64)
-            empty_bank(w, v_grouped[:], v_banks[(w, kt)][:].rearrange("p d t k -> p d k t"))
+            v_grouped = stage.tile([P, BANK_BF16], BF16, align_bytes=64)
+            empty_bank(w, v_grouped[:], v_banks[(w, kt)][:].rearrange("p d q r t -> p (d q r t)"))
             nc.vector.quantize_mx(
                 out=v_codes[w][:, kt].rearrange("p d k -> p (d k)").bitcast(FP8X4),
                 scales=v_scales[w][:, kt].rearrange("p d k -> p (d k)"),
-                in_=v_grouped[:].rearrange("p d k t -> p (d k t)"),
+                in_=v_grouped[:],
             )
 
         x_grouped = {}
@@ -208,13 +219,14 @@ def tile_rnadeoutputlayer_t_kernel(
 
         def transpose_x_bank(n):
             chunk, d, half = x_bank_place(n)
-            bank = tp_psum.tile([P, X_ROWS, PACK, P], BF16, tag="bank")
-            for r in range(X_ROWS):
-                for t in range(PACK):
+            half_blocks = BLOCKS // 2
+            bank = tp_psum.tile([P, half_blocks, ROWS, PACK, PACK], BF16, tag="bank")
+            for j in range(half_blocks):
+                for r in range(PACK):
                     nc.tensor.transpose(
-                        out=bank[:, r, t, :],
-                        in_=x_raws[chunk][:, half * X_ROWS + r, :, t, d],
-                        identity=ident_bf16[:],
+                        out=bank[:, j, :, r, :],
+                        in_=x_raws[chunk][:, half * half_blocks + j, r, :, d],
+                        identity=perm[:],
                     )
             x_banks[n] = bank
 
@@ -222,9 +234,9 @@ def tile_rnadeoutputlayer_t_kernel(
             chunk, d, half = x_bank_place(n)
             if half == 0:
                 x_grouped[(chunk, d)] = stage.tile(
-                    [P, 2, X_ROWS, P, PACK], BF16, name="x_grouped", align_bytes=64
+                    [P, 2, BANK_BF16], BF16, name="x_grouped", align_bytes=64
                 )
-            empty_bank(n, x_grouped[(chunk, d)][:, half], x_banks[n][:].rearrange("p r t b -> p r b t"))
+            empty_bank(n, x_grouped[(chunk, d)][:, half, :], x_banks[n][:].rearrange("p j q r t -> p (j q r t)"))
 
         def quantise_x(g):
             group = (g // D, g % D)
@@ -233,7 +245,7 @@ def tile_rnadeoutputlayer_t_kernel(
             nc.vector.quantize_mx(
                 out=x_codes[group][:].bitcast(FP8X4),
                 scales=x_scales[group][:],
-                in_=x_grouped[group][:].rearrange("p h r b t -> p (h r b t)"),
+                in_=x_grouped[group][:].rearrange("p h c -> p (h c)"),
             )
 
         acc = {}

@@ -16,11 +16,8 @@ AXIS = mybir.AxisListType
 
 P = 128
 PACK = 4
-B, K, H, D = 2048, 512, 512, 2
-H_LOW = H // PACK
-ROWS = P // PACK
 RUN = 8
-BLOCKS_32 = H // 32
+B, K, H, D = 2048, 512, 512, 2
 N_COLS = 512
 BANK_BF16 = 1024
 KT = K // P
@@ -28,10 +25,12 @@ N_CHUNKS = B // N_COLS
 BLOCKS = N_COLS // P
 STEPS = N_CHUNKS * D * KT
 X_BANKS = 2 * D
-LAG_T = KT + 3
-LAG_A = KT + 1
+ROWS = P // PACK
+LAG_T = 6
+LAG_A = 4
 CLIP = 20.0
 SIGMA, MU, ALPHA = 0, 1, 2
+Y_ROW = 16
 
 FLOPS = 2 * B * K * H * D * 3
 
@@ -46,69 +45,71 @@ def tile_rnadeoutputlayer_t_kernel(
     with ExitStack() as ctx:
         const = ctx.enter_context(tc.tile_pool(name="const", bufs=1))
         raw = ctx.enter_context(tc.tile_pool(name="raw", bufs=1))
+        word_pool = ctx.enter_context(tc.tile_pool(name="words", bufs=6))
         stage = ctx.enter_context(tc.tile_pool(name="stage", bufs=3))
         work = ctx.enter_context(tc.tile_pool(name="work", bufs=4))
         keep = ctx.enter_context(tc.tile_pool(name="keep", bufs=3 * KT))
         mx_psum = ctx.enter_context(tc.psum_pool(name="mx_psum", bufs=1))
-        tp_psum = ctx.enter_context(tc.psum_pool(name="tp_psum", bufs=4))
+        tp_psum = ctx.enter_context(tc.psum_pool(name="tp_psum", bufs=5))
         ctx.enter_context(tc.manual_schedule())
 
-        def quarter_rows(a):
-            return a.rearrange("b h d -> (b h d)").rearrange(
-                "(j q m t e) -> j t q m e", q=ROWS, m=PACK * BLOCKS_32, t=PACK, e=RUN * D
-            )
+        def load_whole_rows(rows, name):
+            tile_ = raw.tile([P, H * D], BF16, name=name)
+            nc.sync.dma_start(out=tile_[:], in_=rows.rearrange("r h d -> r (h d)"))
+            return tile_
 
-        x_quarters = quarter_rows(x)
+        x_quarters = x.rearrange("b h d -> (b h d)").rearrange(
+            "(j q m t e) -> j t q m e", q=ROWS, m=PACK * (H // (PACK * RUN)), t=PACK, e=RUN * D
+        )
 
-        def load_rows(tile_, quarters):
-            for t in range(PACK):
-                nc.sync.dma_start(
-                    out=tile_[ROWS * t : ROWS * (t + 1)].rearrange("q r (g i) d -> q (r g) (i d)", i=RUN),
-                    in_=quarters[t],
-                )
-
-        def load_x(chunk):
-            x_raw = raw.tile([P, BLOCKS, PACK, H_LOW, D], BF16, name="x_raw%d" % chunk)
+        def load_quarter_rows(chunk):
+            tile_ = raw.tile([P, BLOCKS, PACK, P, D], BF16, name="x_quarters%d" % chunk)
             for j in range(BLOCKS):
-                load_rows(x_raw[:, j], x_quarters[chunk * BLOCKS + j])
-            return x_raw
+                for t in range(PACK):
+                    nc.sync.dma_start(
+                        out=tile_[ROWS * t : ROWS * (t + 1), j].rearrange(
+                            "q r (g i) d -> q (r g) (i d)", i=RUN
+                        ),
+                        in_=x_quarters[chunk * BLOCKS + j, t],
+                    )
+            return tile_
 
-        def load_weight(w, kt):
-            v_raw = raw.tile([P, PACK, H_LOW, D], BF16, name="v_raw%d_%d" % (w, kt))
-            load_rows(v_raw, quarter_rows(weights[w])[kt])
-            return v_raw
-
-        v_raws = {}
-        x_raws = {}
-        x_raws[0] = load_x(0)
-        for kt in range(KT):
-            for w in (SIGMA, MU, ALPHA):
-                v_raws[(w, kt)] = load_weight(w, kt)
-        for chunk in range(1, N_CHUNKS):
-            x_raws[chunk] = load_x(chunk)
-
-        bias_rows = const.tile([P, P, D], BF16)
-        nc.vector.memset(bias_rows[:], 0.0)
+        small_rows = const.tile([P, P, D], BF16)
+        nc.vector.memset(small_rows[:], 0.0)
         for w in (SIGMA, MU, ALPHA):
             nc.scalar.dma_start(
-                out=bias_rows[KT * w : KT * (w + 1)].rearrange("kt kl d -> kt (kl d)"),
+                out=small_rows[KT * w : KT * (w + 1)].rearrange("kt kl d -> kt (kl d)"),
                 in_=biases[w].rearrange("(kt kl) d -> kt (kl d)", kt=KT),
             )
-        y_row = const.tile([P, B * D], BF16)
-        nc.vector.memset(y_row[:].bitcast(I32), 0)
-        nc.scalar.dma_start(out=y_row[0:1, :], in_=input_var.rearrange("(o b) d -> o (b d)", o=1))
+        n_blocks = B // P
+        nc.scalar.dma_start(
+            out=small_rows[Y_ROW : Y_ROW + n_blocks].rearrange("j b d -> j (b d)"),
+            in_=input_var.rearrange("(j b) d -> j (b d)", j=n_blocks),
+        )
+        sigma_row = const.tile([P, K * D], BF16)
+        nc.gpsimd.memset(sigma_row[:].bitcast(I32), 0)
+        nc.scalar.dma_start(out=sigma_row[0:1, :], in_=b_sigma.rearrange("(o k) d -> o (k d)", o=1))
+
+        x_raws = [load_whole_rows(x[j * P : (j + 1) * P], "x_raw%d" % j) for j in range(BLOCKS)]
+        v_raws = {}
+        for kt in range(KT):
+            for w in (SIGMA, MU, ALPHA):
+                v_raws[(w, kt)] = load_whole_rows(
+                    weights[w][kt * P : (kt + 1) * P], "v_raw%d_%d" % (w, kt)
+                )
+        x_quarter_tiles = {}
+        for chunk in range(1, N_CHUNKS):
+            x_quarter_tiles[chunk] = load_quarter_rows(chunk)
 
         ident_bf16 = const.tile([P, P], BF16)
         make_identity(nc, ident_bf16[:])
         ident_f32 = const.tile([P, P], F32)
         make_identity(nc, ident_f32[:])
-
         perm = const.tile([P, P], BF16)
         nc.vector.tensor_copy(
             out=perm[:].rearrange("p (q t) -> p t q", t=PACK),
             in_=ident_bf16[:].rearrange("p (t q) -> p t q", t=PACK),
         )
-
         ones = const.tile([P, P], BF16)
         nc.vector.memset(ones[:], 1.0)
 
@@ -119,37 +120,67 @@ def tile_rnadeoutputlayer_t_kernel(
         result = const.tile([P, P], F32)
         nc.vector.memset(result[:], 0.0)
 
-        bias = const.tile([P, D, 3 * KT], F32)
-        neg_b_sig = const.tile([P, D, KT], F32)
+        n_small = Y_ROW + n_blocks
+        small = const.tile([P, D, n_small], BF16)
+        b_mu_cols = const.tile([P, D, KT], F32)
+        neg_b_alp = const.tile([P, D, KT], F32)
+        exp_bias = const.tile([P, D, KT], F32)
         clip_low = const.tile([P, D, KT], F32)
         clip_high = const.tile([P, D, KT], F32)
-        b_alp_sig = const.tile([P, D, KT], F32)
-        bias_banks = {}
+        sigma_bias = const.tile([P, D, K], BF16)
+        small_bank = {}
 
-        def transpose_biases():
-            bias_banks[0] = tp_psum.tile([P, D, P], BF16, name="bias_bank", tag="bank")
+        def transpose_small():
+            small_bank[0] = tp_psum.tile([P, D, P], BF16, name="small_bank", tag="bank")
             for d in range(D):
                 nc.tensor.transpose(
-                    out=bias_banks[0][:, d, :], in_=bias_rows[:, :, d], identity=ident_bf16[:]
+                    out=small_bank[0][:, d, :], in_=small_rows[:, :, d], identity=ident_bf16[:]
                 )
 
         def bias_columns():
-            nc.vector.tensor_copy(out=bias[:], in_=bias_banks[0][:, :, 0 : 3 * KT])
-            b_sig = bias[:, :, KT * SIGMA : KT * (SIGMA + 1)]
-            b_alp = bias[:, :, KT * ALPHA : KT * (ALPHA + 1)]
-            nc.vector.tensor_scalar(
-                out=neg_b_sig[:], in0=b_sig, scalar1=-1.0, scalar2=None, op0=ALU.mult
-            )
+            nc.vector.tensor_copy(out=small[:], in_=small_bank[0][:, :, 0:n_small])
+            b_sig = small[:, :, KT * SIGMA : KT * (SIGMA + 1)]
             nc.vector.tensor_scalar(
                 out=clip_low[:], in0=b_sig, scalar1=-1.0, scalar2=-CLIP, op0=ALU.mult, op1=ALU.add
             )
             nc.vector.tensor_scalar(
                 out=clip_high[:], in0=b_sig, scalar1=-1.0, scalar2=CLIP, op0=ALU.mult, op1=ALU.add
             )
-            nc.vector.tensor_tensor(out=b_alp_sig[:], in0=b_alp, in1=b_sig, op=ALU.subtract)
+            nc.vector.tensor_scalar(
+                out=exp_bias[:], in0=b_sig, scalar1=-1.0, scalar2=-0.5 * math.log(2.0),
+                op0=ALU.mult, op1=ALU.add,
+            )
+            nc.vector.tensor_copy(out=b_mu_cols[:], in_=small[:, :, KT * MU : KT * (MU + 1)])
+            nc.vector.tensor_scalar(
+                out=neg_b_alp[:], in0=small[:, :, KT * ALPHA : KT * (ALPHA + 1)],
+                scalar1=-1.0, scalar2=None, op0=ALU.mult,
+            )
 
-        n_blocks = B // P
-        neg_max = const.tile([P, 2, D, n_blocks], F32)
+        def spread_sigma_bias():
+            nc.gpsimd.tensor_copy(
+                out=sigma_bias[:], in_=sigma_row[:].rearrange("p (k d) -> p d k", d=D)
+            )
+
+        y_banks = {}
+        y_all = [const.tile([P, D, N_COLS], BF16, name="y_all%d" % chunk) for chunk in range(N_CHUNKS)]
+
+        def spread_y(chunk):
+            y_banks[chunk] = tp_psum.tile([P, D, BLOCKS, P], BF16, name="y_bank", tag="bank")
+            for d in range(D):
+                for j in range(BLOCKS):
+                    column = Y_ROW + chunk * BLOCKS + j
+                    nc.tensor.transpose(
+                        out=y_banks[chunk][:, d, j, :],
+                        in_=small[:, d, column : column + 1].to_broadcast([P, P]),
+                        identity=ident_bf16[:],
+                    )
+
+        def keep_y(chunk):
+            nc.vector.tensor_copy(
+                out=y_all[chunk][:], in_=y_banks[chunk][:].rearrange("p d j b -> p d (j b)")
+            )
+
+        low = const.tile([P, 2, D, n_blocks], F32)
         exp_sum = const.tile([P, 2, D, n_blocks], F32)
 
         v_codes = [
@@ -159,60 +190,65 @@ def tile_rnadeoutputlayer_t_kernel(
             const.tile([P, KT, D, P], U8, name="v_scales%d" % w, align_bytes=64) for w in range(3)
         ]
 
-        def empty_bank(n, grouped_part, bank):
-            if n % 2 == 0:
-                nc.vector.tensor_copy(out=grouped_part, in_=bank)
+        def copy_on(engine, out, in_):
+            if engine == 0:
+                nc.vector.tensor_copy(out=out, in_=in_)
             else:
-                nc.scalar.copy(out=grouped_part, in_=bank)
+                nc.scalar.copy(out=out, in_=in_)
 
-        y_banks = {}
-        y_all = [const.tile([P, D, N_COLS], BF16, name="y_all%d" % chunk) for chunk in range(N_CHUNKS)]
+        def order_words(raw_tile):
+            words = word_pool.tile([P, PACK, P], F32, name="words")
+            nc.vector.tensor_copy(
+                out=words[:].rearrange("p t (g i) -> p t g i", i=RUN),
+                in_=raw_tile[:].bitcast(F32).rearrange("p (g t i) -> p t g i", t=PACK, i=RUN),
+            )
+            return words
 
-        def spread_y(chunk):
-            for half in range(2):
-                first = (2 * chunk + half) * N_COLS
-                y_banks[(chunk, half)] = tp_psum.tile([P, N_COLS], F32, name="y_bank", tag="bank")
-                nc.tensor.matmul(
-                    out=y_banks[(chunk, half)][:],
-                    lhsT=ones[:],
-                    rhs=y_row[:, first : first + N_COLS],
-                    start=True,
-                    stop=True,
-                )
+        def transpose_words(words):
+            bank = tp_psum.tile([P, PACK, P], F32, name="word_bank", tag="bank")
+            for t in range(PACK):
+                nc.tensor.transpose(out=bank[:, t, :], in_=words[:, t, :], identity=ident_f32[:])
+            return bank
 
-        def keep_y(chunk):
-            samples = N_COLS // D
-            for half in range(2):
-                empty_bank(
-                    half,
-                    y_all[chunk][:, :, half * samples : (half + 1) * samples],
-                    y_banks[(chunk, half)][:].rearrange("p (b d) -> p d b", d=D),
-                )
+        def halves(bank):
+            return (
+                bank[:]
+                .rearrange("p t r -> p (t r)")
+                .bitcast(BF16)
+                .rearrange("p (t r d) -> p d r t", t=PACK, d=D)
+            )
 
+        v_words = {}
         v_banks = {}
-        x_banks = {}
+        v_grouped = {}
+
+        def order_weight(w, kt):
+            v_words[(w, kt)] = order_words(v_raws[(w, kt)])
 
         def transpose_weight(w, kt):
-            bank = tp_psum.tile([P, D, ROWS, PACK, PACK], BF16, tag="bank")
-            for d in range(D):
-                for r in range(PACK):
-                    nc.tensor.transpose(
-                        out=bank[:, d, :, r, :], in_=v_raws[(w, kt)][:, r, :, d], identity=perm[:]
-                    )
-            v_banks[(w, kt)] = bank
+            v_banks[(w, kt)] = transpose_words(v_words[(w, kt)])
+
+        def group_weight(w, kt):
+            v_grouped[(w, kt)] = stage.tile([P, D, P, PACK], BF16, name="v_grouped", align_bytes=64)
+            copy_on((w + kt) % 2, v_grouped[(w, kt)][:], halves(v_banks[(w, kt)]))
 
         def quantise_weight(w, kt):
-            v_grouped = stage.tile([P, BANK_BF16], BF16, align_bytes=64)
-            empty_bank(w, v_grouped[:], v_banks[(w, kt)][:].rearrange("p d q r t -> p (d q r t)"))
             nc.vector.quantize_mx(
                 out=v_codes[w][:, kt].rearrange("p d k -> p (d k)").bitcast(FP8X4),
                 scales=v_scales[w][:, kt].rearrange("p d k -> p (d k)"),
-                in_=v_grouped[:],
+                in_=v_grouped[(w, kt)][:].rearrange("p d k t -> p (d k t)"),
             )
 
         x_grouped = {}
         x_codes = {}
         x_scales = {}
+        x_words = {}
+        x_banks = {}
+
+        def group_tile(group):
+            x_grouped[group] = stage.tile(
+                [P, 2, BANK_BF16], BF16, name="x_grouped", align_bytes=64
+            )
 
         def x_bank_place(n):
             return n // X_BANKS, (n % X_BANKS) // 2, n % 2
@@ -220,12 +256,12 @@ def tile_rnadeoutputlayer_t_kernel(
         def transpose_x_bank(n):
             chunk, d, half = x_bank_place(n)
             half_blocks = BLOCKS // 2
-            bank = tp_psum.tile([P, half_blocks, ROWS, PACK, PACK], BF16, tag="bank")
+            bank = tp_psum.tile([P, half_blocks, ROWS, PACK, PACK], BF16, name="x_bank", tag="bank")
             for j in range(half_blocks):
                 for r in range(PACK):
                     nc.tensor.transpose(
                         out=bank[:, j, :, r, :],
-                        in_=x_raws[chunk][:, half * half_blocks + j, r, :, d],
+                        in_=x_quarter_tiles[chunk][:, half * half_blocks + j, r, :, d],
                         identity=perm[:],
                     )
             x_banks[n] = bank
@@ -233,10 +269,12 @@ def tile_rnadeoutputlayer_t_kernel(
         def empty_x_bank(n):
             chunk, d, half = x_bank_place(n)
             if half == 0:
-                x_grouped[(chunk, d)] = stage.tile(
-                    [P, 2, BANK_BF16], BF16, name="x_grouped", align_bytes=64
-                )
-            empty_bank(n, x_grouped[(chunk, d)][:, half, :], x_banks[n][:].rearrange("p j q r t -> p (j q r t)"))
+                group_tile((chunk, d))
+            copy_on(
+                n % 2,
+                x_grouped[(chunk, d)][:, half, :],
+                x_banks[n][:].rearrange("p j q r t -> p (j q r t)"),
+            )
 
         def quantise_x(g):
             group = (g // D, g % D)
@@ -254,18 +292,17 @@ def tile_rnadeoutputlayer_t_kernel(
         distance = {}
         z = {}
         half_z2 = {}
-        penalty = {}
-        kept = {}
+        neg_a = {}
         turned = {}
 
         def place(step):
             return step // (D * KT), (step // KT) % D, step % KT
 
-        def product(w, step, use=""):
+        def product(w, step):
             chunk, d, kt = place(step)
-            acc[(w, step, use)] = mx_psum.tile([P, N_COLS], F32, name="acc%d%s" % (w, use))
+            acc[(w, step)] = mx_psum.tile([P, N_COLS], F32, name="acc%d" % w)
             nc.tensor.matmul_mx(
-                out=acc[(w, step, use)][:],
+                out=acc[(w, step)][:],
                 lhsT=v_codes[w][:, kt, d, :].bitcast(FP8X4),
                 lhsT_scale=v_scales[w][:, kt, d, :],
                 rhs=x_codes[(chunk, d)][:].bitcast(FP8X4),
@@ -276,10 +313,10 @@ def tile_rnadeoutputlayer_t_kernel(
 
         def clip_log_sigma(step):
             chunk, d, kt = place(step)
-            clipped[step] = work.tile([P, N_COLS], F32, name="clipped")
+            clipped[step] = keep.tile([P, N_COLS], F32, name="clipped")
             nc.vector.tensor_scalar(
                 out=clipped[step][:],
-                in0=acc[(SIGMA, step, "")][:],
+                in0=acc[(SIGMA, step)][:],
                 scalar1=clip_low[:, d, kt : kt + 1],
                 scalar2=clip_high[:, d, kt : kt + 1],
                 op0=ALU.max,
@@ -293,7 +330,7 @@ def tile_rnadeoutputlayer_t_kernel(
                 out=inv_sigma[step][:],
                 in_=clipped[step][:],
                 func=ACT.Exp,
-                bias=neg_b_sig[:, d, kt : kt + 1],
+                bias=exp_bias[:, d, kt : kt + 1],
                 scale=-1.0,
             )
 
@@ -302,8 +339,8 @@ def tile_rnadeoutputlayer_t_kernel(
             distance[step] = work.tile([P, N_COLS], F32, name="distance")
             nc.vector.scalar_tensor_tensor(
                 out=distance[step][:],
-                in0=acc[(MU, step, "")][:],
-                scalar=bias[:, d, KT * MU + kt : KT * MU + kt + 1],
+                in0=acc[(MU, step)][:],
+                scalar=b_mu_cols[:, d, kt : kt + 1],
                 in1=y_all[chunk][:, d, :],
                 op0=ALU.add,
                 op1=ALU.subtract,
@@ -316,38 +353,18 @@ def tile_rnadeoutputlayer_t_kernel(
             )
 
         def square(step):
-            half_z2[step] = work.tile([P, N_COLS], F32, name="half_z2")
-            nc.scalar.activation(
-                out=half_z2[step][:], in_=z[step][:], func=ACT.Square, scale=math.sqrt(0.5)
-            )
+            half_z2[step] = keep.tile([P, N_COLS], F32, name="half_z2")
+            nc.gpsimd.tensor_tensor(out=half_z2[step][:], in0=z[step][:], in1=z[step][:], op=ALU.mult)
 
-        def add_penalty(step):
-            penalty[step] = work.tile([P, N_COLS], F32, name="penalty")
-            nc.gpsimd.tensor_tensor(
-                out=penalty[step][:], in0=clipped[step][:], in1=half_z2[step][:], op=ALU.add
-            )
-
-        def make_a(step):
+        def make_neg_a(step):
             chunk, d, kt = place(step)
-            kept[(1, step)] = keep.tile([P, N_COLS], F32, name="a_tile")
+            neg_a[step] = keep.tile([P, N_COLS], F32, name="neg_a")
             nc.scalar.activation(
-                out=kept[(1, step)][:],
-                in_=acc[(ALPHA, step, "a")][:],
+                out=neg_a[step][:],
+                in_=acc[(ALPHA, step)][:],
                 func=ACT.Identity,
-                bias=bias[:, d, KT * ALPHA + kt : KT * ALPHA + kt + 1],
-                scale=1.0,
-            )
-
-        def make_t(step):
-            chunk, d, kt = place(step)
-            kept[(0, step)] = keep.tile([P, N_COLS], F32, name="t_tile")
-            nc.vector.scalar_tensor_tensor(
-                out=kept[(0, step)][:],
-                in0=acc[(ALPHA, step, "t")][:],
-                scalar=b_alp_sig[:, d, kt : kt + 1],
-                in1=penalty[step][:],
-                op0=ALU.add,
-                op1=ALU.subtract,
+                bias=neg_b_alp[:, d, kt : kt + 1],
+                scale=-1.0,
             )
 
         def statistic(tile_, kind, block):
@@ -355,34 +372,52 @@ def tile_rnadeoutputlayer_t_kernel(
             column = chunk * BLOCKS + j
             return tile_[:, kind, d, column : column + 1]
 
-        def turn(kind, block):
+        def turn_a(block):
             first_step = (block // BLOCKS) * KT
             j = block % BLOCKS
-            turned[(kind, block)] = tp_psum.tile([P, K], F32, name="turned", tag="bank")
+            turned[(1, block)] = tp_psum.tile([P, K], F32, name="turned_a", tag="bank")
             for kt in range(KT):
                 nc.tensor.transpose(
-                    out=turned[(kind, block)][:, kt * P : (kt + 1) * P],
-                    in_=kept[(kind, first_step + kt)][:, j * P : (j + 1) * P],
+                    out=turned[(1, block)][:, kt * P : (kt + 1) * P],
+                    in_=neg_a[first_step + kt][:, j * P : (j + 1) * P],
                     identity=ident_f32[:],
                 )
 
-        def maximum(kind, block):
+        def turn_t(block):
+            first_step = (block // BLOCKS) * KT
+            d = (block // BLOCKS) % D
+            j = block % BLOCKS
+            turned[(0, block)] = tp_psum.tile([P, K], F32, name="turned_t", tag="bank")
+            nc.tensor.matmul(
+                out=turned[(0, block)][:], lhsT=ones[:], rhs=sigma_bias[:, d, :], start=True, stop=False
+            )
+            for parts in (neg_a, clipped, half_z2):
+                for kt in range(KT):
+                    nc.tensor.matmul(
+                        out=turned[(0, block)][:, kt * P : (kt + 1) * P],
+                        lhsT=parts[first_step + kt][:, j * P : (j + 1) * P],
+                        rhs=ident_f32[:],
+                        start=False,
+                        stop=(parts is half_z2 and kt == KT - 1),
+                        is_transpose=True,
+                    )
+
+        def minimum(kind, block):
             nc.vector.tensor_reduce(
-                out=statistic(neg_max, kind, block),
+                out=statistic(low, kind, block),
                 in_=turned[(kind, block)][:],
                 axis=AXIS.X,
-                op=ALU.max,
-                negate=True,
+                op=ALU.min,
             )
 
         def sum_of_exp(kind, block):
-            unread = work.tile([P, K], F32)
+            unread = work.tile([P, K], F32, name="unread")
             nc.scalar.activation(
                 out=unread[:],
                 in_=turned[(kind, block)][:],
                 func=ACT.Exp,
-                bias=statistic(neg_max, kind, block),
-                scale=1.0,
+                bias=statistic(low, kind, block),
+                scale=-1.0,
                 accum_out=statistic(exp_sum, kind, block),
             )
 
@@ -394,79 +429,93 @@ def tile_rnadeoutputlayer_t_kernel(
         def is_block(block):
             return 0 <= block < STEPS
 
-        transpose_x_bank(0)
-        transpose_x_bank(1)
+        for j in range(BLOCKS):
+            x_words[j] = order_words(x_raws[j])
+        for j in range(BLOCKS):
+            x_banks[j] = transpose_words(x_words[j])
+        for d in range(D):
+            group_tile((0, d))
+        order_weight(SIGMA, 0)
+        for d in range(D):
+            for j in range(BLOCKS):
+                grouped = x_grouped[(0, d)][:, j // 2].rearrange("p (j b t) -> p j b t", j=2, t=PACK)
+                copy_on(j % 2, grouped[:, j % 2], halves(x_banks[j])[:, d])
+            if d == 0:
+                quantise_x(0)
         transpose_weight(SIGMA, 0)
-        transpose_biases()
-        empty_x_bank(0)
-        empty_x_bank(1)
-        quantise_weight(SIGMA, 0)
-        quantise_x(0)
-        bias_columns()
+        order_weight(MU, 0)
+        group_weight(SIGMA, 0)
+        transpose_small()
         transpose_weight(MU, 0)
+        quantise_weight(SIGMA, 0)
+        bias_columns()
+        spread_sigma_bias()
+        order_weight(ALPHA, 0)
         spread_y(0)
+        group_weight(MU, 0)
+        transpose_weight(ALPHA, 0)
         quantise_weight(MU, 0)
         keep_y(0)
         product(SIGMA, 0)
         product(MU, 0)
-        transpose_weight(ALPHA, 0)
+        group_weight(ALPHA, 0)
+        for w in (SIGMA, MU, ALPHA):
+            order_weight(w, 1)
         quantise_weight(ALPHA, 0)
+        product(ALPHA, 0)
         for w in (SIGMA, MU, ALPHA):
             transpose_weight(w, 1)
-        transpose_x_bank(2)
 
         for i in range(STEPS + LAG_T + 2):
             if is_block(i - LAG_T):
-                turn(0, i - LAG_T)
+                turn_t(i - LAG_T)
             if is_block(i - LAG_A):
-                turn(1, i - LAG_A)
+                turn_a(i - LAG_A)
+            if is_step(i):
+                clip_log_sigma(i)
+                make_neg_a(i)
+                mu_minus_y(i)
             if is_step(i - 2):
                 square(i - 2)
             if is_step(i - 1):
-                make_a(i - 1)
-            if is_step(i):
-                clip_log_sigma(i)
-                mu_minus_y(i)
+                divide_by_sigma(i - 1)
 
             if i + 1 < KT:
                 for w in (SIGMA, MU, ALPHA):
+                    group_weight(w, i + 1)
+                for w in (SIGMA, MU, ALPHA):
                     quantise_weight(w, i + 1)
-            if i % 2 == 0 and (i + 4) // 2 < n_x_banks:
+            if i + 2 < KT:
+                for w in (SIGMA, MU, ALPHA):
+                    order_weight(w, i + 2)
+            if i == 0:
+                quantise_x(1)
+            if i % 2 == 0 and X_BANKS <= (i + 4) // 2 < n_x_banks:
                 empty_x_bank((i + 4) // 2)
             if 1 <= i - 2 < N_CHUNKS:
                 keep_y(i - 2)
 
-            if is_step(i - 3):
-                make_t(i - 3)
             if is_step(i + 1):
-                product(SIGMA, i + 1)
-                product(MU, i + 1)
-            if is_step(i):
-                product(ALPHA, i, "a")
-            if is_step(i - 2):
-                product(ALPHA, i - 2, "t")
-            if is_step(i - 1):
-                divide_by_sigma(i - 1)
-            if is_step(i - 2):
-                add_penalty(i - 2)
+                for w in (SIGMA, MU, ALPHA):
+                    product(w, i + 1)
 
             if is_block(i - LAG_T):
-                maximum(0, i - LAG_T)
+                minimum(0, i - LAG_T)
             if is_block(i - LAG_A):
-                maximum(1, i - LAG_A)
-            if i % 4 == 2 and 1 <= (i + 2) // 4 < N_CHUNKS * D:
+                minimum(1, i - LAG_A)
+            if i % 4 == 2 and D <= (i + 2) // 4 < N_CHUNKS * D:
                 quantise_x((i + 2) // 4)
+            if is_step(i):
+                exp_minus_log_sigma(i)
             if is_block(i - LAG_T - 1):
                 sum_of_exp(0, i - LAG_T - 1)
             if is_block(i - LAG_A - 1):
                 sum_of_exp(1, i - LAG_A - 1)
-            if is_step(i):
-                exp_minus_log_sigma(i)
 
             if i + 2 < KT:
                 for w in (SIGMA, MU, ALPHA):
                     transpose_weight(w, i + 2)
-            if i % 2 == 1 and (i + 5) // 2 < n_x_banks:
+            if i % 2 == 1 and X_BANKS <= (i + 5) // 2 < n_x_banks:
                 transpose_x_bank((i + 5) // 2)
             if 1 <= i - 1 < N_CHUNKS:
                 spread_y(i - 1)
@@ -474,7 +523,7 @@ def tile_rnadeoutputlayer_t_kernel(
         log_sum = const.tile([P, 2, D, n_blocks], F32)
         nc.scalar.activation(out=log_sum[:], in_=exp_sum[:], func=ACT.Ln)
         lse = const.tile([P, 2, D, n_blocks], F32)
-        nc.vector.tensor_tensor(out=lse[:], in0=log_sum[:], in1=neg_max[:], op=ALU.subtract)
+        nc.vector.tensor_tensor(out=lse[:], in0=log_sum[:], in1=low[:], op=ALU.subtract)
         per_d = const.tile([P, D, n_blocks], F32)
         nc.vector.tensor_tensor(out=per_d[:], in0=lse[:, 0], in1=lse[:, 1], op=ALU.subtract)
         nc.vector.scalar_tensor_tensor(
@@ -485,7 +534,7 @@ def tile_rnadeoutputlayer_t_kernel(
             op0=ALU.add,
             op1=ALU.add,
         )
-        result_bank = tp_psum.tile([P, P], F32, tag="bank")
+        result_bank = tp_psum.tile([P, P], F32, name="result_bank", tag="bank")
         nc.tensor.transpose(out=result_bank[:], in_=result[:], identity=ident_f32[:])
         out_rows = const.tile([n_blocks, P], F32)
         nc.scalar.copy(out=out_rows[:], in_=result_bank[0:n_blocks, :])

@@ -26,11 +26,14 @@ BLOCKS = N_COLS // P
 STEPS = N_CHUNKS * D * KT
 X_BANKS = 2 * D
 ROWS = P // PACK
-LAG_T = 6
+LAG_T = 5
 LAG_A = 4
+VECTOR_A = (1, 3)
 CLIP = 20.0
 SIGMA, MU, ALPHA = 0, 1, 2
-Y_ROW = 16
+VECTOR, SCALAR = 0, 1
+X_ENGINE = SCALAR
+N_BLOCKS = B // P
 
 FLOPS = 2 * B * K * H * D * 3
 
@@ -45,32 +48,31 @@ def tile_rnadeoutputlayer_t_kernel(
     with ExitStack() as ctx:
         const = ctx.enter_context(tc.tile_pool(name="const", bufs=1))
         raw = ctx.enter_context(tc.tile_pool(name="raw", bufs=1))
-        word_pool = ctx.enter_context(tc.tile_pool(name="words", bufs=6))
+        word_pool = ctx.enter_context(tc.tile_pool(name="words", bufs=KT + 3 * KT))
         stage = ctx.enter_context(tc.tile_pool(name="stage", bufs=3))
         work = ctx.enter_context(tc.tile_pool(name="work", bufs=4))
         keep = ctx.enter_context(tc.tile_pool(name="keep", bufs=3 * KT))
         mx_psum = ctx.enter_context(tc.psum_pool(name="mx_psum", bufs=1))
-        tp_psum = ctx.enter_context(tc.psum_pool(name="tp_psum", bufs=5))
+        turn_psum = ctx.enter_context(tc.psum_pool(name="turn_psum", bufs=3))
+        in_psum = ctx.enter_context(tc.psum_pool(name="in_psum", bufs=2))
         ctx.enter_context(tc.manual_schedule())
 
-        def load_whole_rows(rows, name):
-            tile_ = raw.tile([P, H * D], BF16, name=name)
-            nc.sync.dma_start(out=tile_[:], in_=rows.rearrange("r h d -> r (h d)"))
-            return tile_
+        x_blocks = x.rearrange("(p j) h d -> j p (h d)", j=N_BLOCKS)
 
         x_quarters = x.rearrange("b h d -> (b h d)").rearrange(
-            "(j q m t e) -> j t q m e", q=ROWS, m=PACK * (H // (PACK * RUN)), t=PACK, e=RUN * D
+            "(q r c m t e) -> c r t q m e",
+            q=ROWS, r=PACK, c=N_CHUNKS, m=BLOCKS * (H // (PACK * RUN)), t=PACK, e=RUN * D,
         )
 
         def load_quarter_rows(chunk):
-            tile_ = raw.tile([P, BLOCKS, PACK, P, D], BF16, name="x_quarters%d" % chunk)
-            for j in range(BLOCKS):
+            tile_ = raw.tile([P, PACK, BLOCKS, P, D], BF16, name="x_quarters%d" % chunk)
+            for r in range(PACK):
                 for t in range(PACK):
                     nc.sync.dma_start(
-                        out=tile_[ROWS * t : ROWS * (t + 1), j].rearrange(
-                            "q r (g i) d -> q (r g) (i d)", i=RUN
+                        out=tile_[ROWS * t : ROWS * (t + 1), r].rearrange(
+                            "q j (g i) d -> q (j g) (i d)", i=RUN
                         ),
-                        in_=x_quarters[chunk * BLOCKS + j, t],
+                        in_=x_quarters[chunk, r, t],
                     )
             return tile_
 
@@ -81,25 +83,32 @@ def tile_rnadeoutputlayer_t_kernel(
                 out=small_rows[KT * w : KT * (w + 1)].rearrange("kt kl d -> kt (kl d)"),
                 in_=biases[w].rearrange("(kt kl) d -> kt (kl d)", kt=KT),
             )
-        n_blocks = B // P
+        y_cols = const.tile([P, N_BLOCKS, D], BF16)
         nc.scalar.dma_start(
-            out=small_rows[Y_ROW : Y_ROW + n_blocks].rearrange("j b d -> j (b d)"),
-            in_=input_var.rearrange("(j b) d -> j (b d)", j=n_blocks),
+            out=y_cols[:].rearrange("p j d -> p (j d)"),
+            in_=input_var.rearrange("(p j) d -> p (j d)", j=N_BLOCKS),
         )
         sigma_row = const.tile([P, K * D], BF16)
         nc.gpsimd.memset(sigma_row[:].bitcast(I32), 0)
         nc.scalar.dma_start(out=sigma_row[0:1, :], in_=b_sigma.rearrange("(o k) d -> o (k d)", o=1))
 
-        x_raws = [load_whole_rows(x[j * P : (j + 1) * P], "x_raw%d" % j) for j in range(BLOCKS)]
+        x_raws = []
+        for j in range(BLOCKS):
+            x_raws.append(raw.tile([P, H * D], BF16, name="x_raw%d" % j))
+            nc.sync.dma_start(out=x_raws[j][:], in_=x_blocks[j])
         v_raws = {}
-        for kt in range(KT):
+
+        def load_weights(kt):
             for w in (SIGMA, MU, ALPHA):
-                v_raws[(w, kt)] = load_whole_rows(
-                    weights[w][kt * P : (kt + 1) * P], "v_raw%d_%d" % (w, kt)
+                v_raws[(w, kt)] = raw.tile([P, H * D], BF16, name="v_raw", bufs=9)
+                nc.sync.dma_start(
+                    out=v_raws[(w, kt)][:],
+                    in_=weights[w][kt * P : (kt + 1) * P].rearrange("k h d -> k (h d)"),
                 )
+
+        for kt in range(KT - 1):
+            load_weights(kt)
         x_quarter_tiles = {}
-        for chunk in range(1, N_CHUNKS):
-            x_quarter_tiles[chunk] = load_quarter_rows(chunk)
 
         ident_bf16 = const.tile([P, P], BF16)
         make_identity(nc, ident_bf16[:])
@@ -117,10 +126,7 @@ def tile_rnadeoutputlayer_t_kernel(
         nc.vector.memset(warm[:], 0.0)
         nc.scalar.activation(out=warm[:, 1:2], in_=warm[:, 0:1], func=ACT.Exp)
 
-        result = const.tile([P, P], F32)
-        nc.vector.memset(result[:], 0.0)
-
-        n_small = Y_ROW + n_blocks
+        n_small = 3 * KT
         small = const.tile([P, D, n_small], BF16)
         b_mu_cols = const.tile([P, D, KT], F32)
         neg_b_alp = const.tile([P, D, KT], F32)
@@ -131,7 +137,7 @@ def tile_rnadeoutputlayer_t_kernel(
         small_bank = {}
 
         def transpose_small():
-            small_bank[0] = tp_psum.tile([P, D, P], BF16, name="small_bank", tag="bank")
+            small_bank[0] = turn_psum.tile([P, D, P], BF16, name="small_bank", tag="turn")
             for d in range(D):
                 nc.tensor.transpose(
                     out=small_bank[0][:, d, :], in_=small_rows[:, :, d], identity=ident_bf16[:]
@@ -157,31 +163,31 @@ def tile_rnadeoutputlayer_t_kernel(
             )
 
         def spread_sigma_bias():
-            nc.gpsimd.tensor_copy(
-                out=sigma_bias[:], in_=sigma_row[:].rearrange("p (k d) -> p d k", d=D)
-            )
+            nc.scalar.copy(out=sigma_bias[:], in_=sigma_row[:].rearrange("p (k d) -> p d k", d=D))
 
         y_banks = {}
-        y_all = [const.tile([P, D, N_COLS], BF16, name="y_all%d" % chunk) for chunk in range(N_CHUNKS)]
+        y_all = {}
 
-        def spread_y(chunk):
-            y_banks[chunk] = tp_psum.tile([P, D, BLOCKS, P], BF16, name="y_bank", tag="bank")
-            for d in range(D):
-                for j in range(BLOCKS):
-                    column = Y_ROW + chunk * BLOCKS + j
-                    nc.tensor.transpose(
-                        out=y_banks[chunk][:, d, j, :],
-                        in_=small[:, d, column : column + 1].to_broadcast([P, P]),
-                        identity=ident_bf16[:],
-                    )
+        def spread_y(chunk, d):
+            if chunk == 0:
+                y_banks[(chunk, d)] = turn_psum.tile([P, BLOCKS, P], BF16, name="y_bank", tag="turn")
+            else:
+                y_banks[(chunk, d)] = in_psum.tile([P, BLOCKS, P], BF16, name="y_bank", tag="in")
+            for j in range(BLOCKS):
+                nc.tensor.transpose(
+                    out=y_banks[(chunk, d)][:, j, :],
+                    in_=y_cols[:, chunk * BLOCKS + j, d : d + 1].to_broadcast([P, P]),
+                    identity=ident_bf16[:],
+                )
 
-        def keep_y(chunk):
+        def keep_y(chunk, d):
+            y_all[(chunk, d)] = const.tile([P, N_COLS], BF16, name="y_all%d_%d" % (chunk, d))
             nc.vector.tensor_copy(
-                out=y_all[chunk][:], in_=y_banks[chunk][:].rearrange("p d j b -> p d (j b)")
+                out=y_all[(chunk, d)][:], in_=y_banks[(chunk, d)][:].rearrange("p j b -> p (j b)")
             )
 
-        low = const.tile([P, 2, D, n_blocks], F32)
-        exp_sum = const.tile([P, 2, D, n_blocks], F32)
+        low = const.tile([P, 2, D, N_BLOCKS], F32)
+        exp_sum = const.tile([P, 2, D, N_BLOCKS], F32)
 
         v_codes = [
             const.tile([P, KT, D, P], U32, name="v_codes%d" % w, align_bytes=64) for w in range(3)
@@ -204,18 +210,18 @@ def tile_rnadeoutputlayer_t_kernel(
             )
             return words
 
-        def transpose_words(words):
-            bank = tp_psum.tile([P, PACK, P], F32, name="word_bank", tag="bank")
+        def transpose_words(words, pool, tag):
+            bank = pool.tile([P, PACK, P], F32, name="word_bank", tag=tag)
             for t in range(PACK):
                 nc.tensor.transpose(out=bank[:, t, :], in_=words[:, t, :], identity=ident_f32[:])
             return bank
 
-        def halves(bank):
+        def one_d(bank, d):
             return (
                 bank[:]
                 .rearrange("p t r -> p (t r)")
                 .bitcast(BF16)
-                .rearrange("p (t r d) -> p d r t", t=PACK, d=D)
+                .rearrange("p (t r d) -> p d r t", t=PACK, d=D)[:, d]
             )
 
         v_words = {}
@@ -225,18 +231,21 @@ def tile_rnadeoutputlayer_t_kernel(
         def order_weight(w, kt):
             v_words[(w, kt)] = order_words(v_raws[(w, kt)])
 
-        def transpose_weight(w, kt):
-            v_banks[(w, kt)] = transpose_words(v_words[(w, kt)])
+        def transpose_weight(w, kt, d):
+            if w == ALPHA and d * KT + kt < 6:
+                v_banks[(w, kt, d)] = transpose_words(v_words[(w, kt)], turn_psum, "turn")
+            else:
+                v_banks[(w, kt, d)] = transpose_words(v_words[(w, kt)], in_psum, "in")
 
-        def group_weight(w, kt):
-            v_grouped[(w, kt)] = stage.tile([P, D, P, PACK], BF16, name="v_grouped", align_bytes=64)
-            copy_on((w + kt) % 2, v_grouped[(w, kt)][:], halves(v_banks[(w, kt)]))
+        def group_weight(engine, w, kt, d):
+            v_grouped[(w, kt, d)] = stage.tile([P, P, PACK], BF16, name="v_grouped", align_bytes=64, bufs=6)
+            copy_on(engine, v_grouped[(w, kt, d)][:], one_d(v_banks[(w, kt, d)], d))
 
-        def quantise_weight(w, kt):
+        def quantise_weight(w, kt, d):
             nc.vector.quantize_mx(
-                out=v_codes[w][:, kt].rearrange("p d k -> p (d k)").bitcast(FP8X4),
-                scales=v_scales[w][:, kt].rearrange("p d k -> p (d k)"),
-                in_=v_grouped[(w, kt)][:].rearrange("p d k t -> p (d k t)"),
+                out=v_codes[w][:, kt, d].bitcast(FP8X4),
+                scales=v_scales[w][:, kt, d],
+                in_=v_grouped[(w, kt, d)][:].rearrange("p k t -> p (k t)"),
             )
 
         x_grouped = {}
@@ -247,7 +256,7 @@ def tile_rnadeoutputlayer_t_kernel(
 
         def group_tile(group):
             x_grouped[group] = stage.tile(
-                [P, 2, BANK_BF16], BF16, name="x_grouped", align_bytes=64
+                [P, BLOCKS, P, PACK], BF16, name="x_grouped", align_bytes=64, bufs=2
             )
 
         def x_bank_place(n):
@@ -255,13 +264,13 @@ def tile_rnadeoutputlayer_t_kernel(
 
         def transpose_x_bank(n):
             chunk, d, half = x_bank_place(n)
-            half_blocks = BLOCKS // 2
-            bank = tp_psum.tile([P, half_blocks, ROWS, PACK, PACK], BF16, name="x_bank", tag="bank")
-            for j in range(half_blocks):
-                for r in range(PACK):
+            half_rows = PACK // 2
+            bank = in_psum.tile([P, BLOCKS, ROWS, half_rows, PACK], BF16, name="x_bank", tag="in")
+            for r in range(half_rows):
+                for j in range(BLOCKS):
                     nc.tensor.transpose(
                         out=bank[:, j, :, r, :],
-                        in_=x_quarter_tiles[chunk][:, half * half_blocks + j, r, :, d],
+                        in_=x_quarter_tiles[chunk][:, half * half_rows + r, j, :, d],
                         identity=perm[:],
                     )
             x_banks[n] = bank
@@ -270,10 +279,14 @@ def tile_rnadeoutputlayer_t_kernel(
             chunk, d, half = x_bank_place(n)
             if half == 0:
                 group_tile((chunk, d))
+            half_rows = PACK // 2
             copy_on(
-                n % 2,
-                x_grouped[(chunk, d)][:, half, :],
-                x_banks[n][:].rearrange("p j q r t -> p (j q r t)"),
+                X_ENGINE,
+                x_grouped[(chunk, d)][:]
+                .rearrange("p j (q s) t -> p (j q) (s t)", s=PACK)[
+                    :, :, half * half_rows * PACK : (half + 1) * half_rows * PACK
+                ],
+                x_banks[n][:].rearrange("p j q r t -> p (j q) (r t)"),
             )
 
         def quantise_x(g):
@@ -283,7 +296,7 @@ def tile_rnadeoutputlayer_t_kernel(
             nc.vector.quantize_mx(
                 out=x_codes[group][:].bitcast(FP8X4),
                 scales=x_scales[group][:],
-                in_=x_grouped[group][:].rearrange("p h c -> p (h c)"),
+                in_=x_grouped[group][:].rearrange("p j b t -> p (j b t)"),
             )
 
         acc = {}
@@ -341,24 +354,42 @@ def tile_rnadeoutputlayer_t_kernel(
                 out=distance[step][:],
                 in0=acc[(MU, step)][:],
                 scalar=b_mu_cols[:, d, kt : kt + 1],
-                in1=y_all[chunk][:, d, :],
+                in1=y_all[(chunk, d)][:],
                 op0=ALU.add,
                 op1=ALU.subtract,
             )
 
         def divide_by_sigma(step):
             z[step] = work.tile([P, N_COLS], F32, name="z")
-            nc.gpsimd.tensor_tensor(
+            engine = nc.vector if step == STEPS - 1 else nc.gpsimd
+            engine.tensor_tensor(
                 out=z[step][:], in0=distance[step][:], in1=inv_sigma[step][:], op=ALU.mult
             )
 
         def square(step):
             half_z2[step] = keep.tile([P, N_COLS], F32, name="half_z2")
-            nc.gpsimd.tensor_tensor(out=half_z2[step][:], in0=z[step][:], in1=z[step][:], op=ALU.mult)
+            if step == STEPS - 1:
+                nc.vector.tensor_tensor(
+                    out=half_z2[step][:], in0=z[step][:], in1=z[step][:], op=ALU.mult
+                )
+            else:
+                nc.gpsimd.tensor_tensor(
+                    out=half_z2[step][:], in0=z[step][:], in1=z[step][:], op=ALU.mult
+                )
 
         def make_neg_a(step):
             chunk, d, kt = place(step)
             neg_a[step] = keep.tile([P, N_COLS], F32, name="neg_a")
+            if kt in VECTOR_A:
+                nc.vector.tensor_scalar(
+                    out=neg_a[step][:],
+                    in0=acc[(ALPHA, step)][:],
+                    scalar1=-1.0,
+                    scalar2=neg_b_alp[:, d, kt : kt + 1],
+                    op0=ALU.mult,
+                    op1=ALU.add,
+                )
+                return
             nc.scalar.activation(
                 out=neg_a[step][:],
                 in_=acc[(ALPHA, step)][:],
@@ -372,10 +403,13 @@ def tile_rnadeoutputlayer_t_kernel(
             column = chunk * BLOCKS + j
             return tile_[:, kind, d, column : column + 1]
 
-        def turn_a(block):
+        def turn_a(block, bank=None):
             first_step = (block // BLOCKS) * KT
             j = block % BLOCKS
-            turned[(1, block)] = tp_psum.tile([P, K], F32, name="turned_a", tag="bank")
+            if bank is None:
+                turned[(1, block)] = turn_psum.tile([P, K], F32, name="turned_a", tag="turn")
+            else:
+                turned[(1, block)] = mx_psum.tile([P, K], F32, name="acc%d" % bank)
             for kt in range(KT):
                 nc.tensor.transpose(
                     out=turned[(1, block)][:, kt * P : (kt + 1) * P],
@@ -383,24 +417,32 @@ def tile_rnadeoutputlayer_t_kernel(
                     identity=ident_f32[:],
                 )
 
-        def turn_t(block):
+        def add_turned(block, parts, kts, last):
             first_step = (block // BLOCKS) * KT
-            d = (block // BLOCKS) % D
             j = block % BLOCKS
-            turned[(0, block)] = tp_psum.tile([P, K], F32, name="turned_t", tag="bank")
+            terms = [(part, kt) for part in parts for kt in kts]
+            for n, (part, kt) in enumerate(terms):
+                nc.tensor.matmul(
+                    out=turned[(0, block)][:, kt * P : (kt + 1) * P],
+                    lhsT=part[first_step + kt][:, j * P : (j + 1) * P],
+                    rhs=ident_f32[:],
+                    start=False,
+                    stop=(last and n == len(terms) - 1),
+                    is_transpose=True,
+                )
+
+        def open_t(block):
+            d = (block // BLOCKS) % D
+            if block >= STEPS - 2:
+                turned[(0, block)] = in_psum.tile([P, K], F32, name="turned_t", tag="in")
+            else:
+                turned[(0, block)] = turn_psum.tile([P, K], F32, name="turned_t", tag="turn")
             nc.tensor.matmul(
                 out=turned[(0, block)][:], lhsT=ones[:], rhs=sigma_bias[:, d, :], start=True, stop=False
             )
-            for parts in (neg_a, clipped, half_z2):
-                for kt in range(KT):
-                    nc.tensor.matmul(
-                        out=turned[(0, block)][:, kt * P : (kt + 1) * P],
-                        lhsT=parts[first_step + kt][:, j * P : (j + 1) * P],
-                        rhs=ident_f32[:],
-                        start=False,
-                        stop=(parts is half_z2 and kt == KT - 1),
-                        is_transpose=True,
-                    )
+
+        def turn_t(block):
+            add_turned(block, (neg_a, clipped, half_z2), range(KT), last=True)
 
         def minimum(kind, block):
             nc.vector.tensor_reduce(
@@ -411,7 +453,7 @@ def tile_rnadeoutputlayer_t_kernel(
             )
 
         def sum_of_exp(kind, block):
-            unread = work.tile([P, K], F32, name="unread")
+            unread = work.tile([P, K], F32, name="unread", bufs=2)
             nc.scalar.activation(
                 out=unread[:],
                 in_=turned[(kind, block)][:],
@@ -429,113 +471,193 @@ def tile_rnadeoutputlayer_t_kernel(
         def is_block(block):
             return 0 <= block < STEPS
 
+        def group_x0(engine, j, d):
+            copy_on(engine, x_grouped[(0, d)][:, j], one_d(x_banks[(j, d)], d))
+
+        def weight_half(h):
+            return h % KT, h // KT
+
+        def transpose_half(h):
+            for w in (SIGMA, MU, ALPHA):
+                transpose_weight(w, *weight_half(h))
+
+        def group_half(h):
+            for w in (SIGMA, MU, ALPHA):
+                group_weight(SCALAR, w, *weight_half(h))
+
+        def quantise_half(h):
+            for w in (SIGMA, MU, ALPHA):
+                quantise_weight(w, *weight_half(h))
+
+        halves = D * KT
+
+        x_bank_at = {}
+        for g in range(D, N_CHUNKS * D):
+            for half in range(2):
+                x_bank_at.setdefault(KT * g - KT - 1 + (2 if g == D else 0) + half, []).append(2 * g + half)
+
         for j in range(BLOCKS):
             x_words[j] = order_words(x_raws[j])
+        group_tile((0, 0))
         for j in range(BLOCKS):
-            x_banks[j] = transpose_words(x_words[j])
-        for d in range(D):
-            group_tile((0, d))
+            if j < 2:
+                x_banks[(j, 0)] = transpose_words(x_words[j], in_psum, "in")
+            else:
+                x_banks[(j, 0)] = transpose_words(x_words[j], turn_psum, "turn")
         order_weight(SIGMA, 0)
-        for d in range(D):
-            for j in range(BLOCKS):
-                grouped = x_grouped[(0, d)][:, j // 2].rearrange("p (j b t) -> p j b t", j=2, t=PACK)
-                copy_on(j % 2, grouped[:, j % 2], halves(x_banks[j])[:, d])
-            if d == 0:
-                quantise_x(0)
-        transpose_weight(SIGMA, 0)
+        group_x0(VECTOR, 0, 0)
+        group_x0(SCALAR, 1, 0)
         order_weight(MU, 0)
-        group_weight(SIGMA, 0)
-        transpose_small()
-        transpose_weight(MU, 0)
-        quantise_weight(SIGMA, 0)
-        bias_columns()
-        spread_sigma_bias()
+        group_x0(VECTOR, 2, 0)
+        group_x0(SCALAR, 3, 0)
         order_weight(ALPHA, 0)
-        spread_y(0)
-        group_weight(MU, 0)
-        transpose_weight(ALPHA, 0)
-        quantise_weight(MU, 0)
-        keep_y(0)
+        load_weights(KT - 1)
+        for chunk in range(1, N_CHUNKS):
+            x_quarter_tiles[chunk] = load_quarter_rows(chunk)
+        transpose_weight(SIGMA, 0, 0)
+        transpose_weight(MU, 0, 0)
+        group_weight(SCALAR, SIGMA, 0, 0)
+        quantise_x(0)
+        transpose_small()
+        spread_y(0, 0)
+        group_weight(SCALAR, MU, 0, 0)
+        bias_columns()
+        quantise_weight(SIGMA, 0, 0)
+        transpose_weight(ALPHA, 0, 0)
+        keep_y(0, 0)
         product(SIGMA, 0)
+        quantise_weight(MU, 0, 0)
         product(MU, 0)
-        group_weight(ALPHA, 0)
+        group_weight(SCALAR, ALPHA, 0, 0)
         for w in (SIGMA, MU, ALPHA):
             order_weight(w, 1)
-        quantise_weight(ALPHA, 0)
+        transpose_half(1)
+        quantise_weight(ALPHA, 0, 0)
         product(ALPHA, 0)
         for w in (SIGMA, MU, ALPHA):
-            transpose_weight(w, 1)
+            order_weight(w, 2)
+        group_half(1)
+        transpose_half(2)
 
-        for i in range(STEPS + LAG_T + 2):
-            if is_block(i - LAG_T):
-                turn_t(i - LAG_T)
-            if is_block(i - LAG_A):
-                turn_a(i - LAG_A)
-            if is_step(i):
+        for i in range(STEPS):
+            if i == STEPS - 1:
                 clip_log_sigma(i)
-                make_neg_a(i)
-                mu_minus_y(i)
-            if is_step(i - 2):
-                square(i - 2)
-            if is_step(i - 1):
-                divide_by_sigma(i - 1)
-
-            if i + 1 < KT:
-                for w in (SIGMA, MU, ALPHA):
-                    group_weight(w, i + 1)
-                for w in (SIGMA, MU, ALPHA):
-                    quantise_weight(w, i + 1)
-            if i + 2 < KT:
-                for w in (SIGMA, MU, ALPHA):
-                    order_weight(w, i + 2)
-            if i == 0:
-                quantise_x(1)
-            if i % 2 == 0 and X_BANKS <= (i + 4) // 2 < n_x_banks:
-                empty_x_bank((i + 4) // 2)
-            if 1 <= i - 2 < N_CHUNKS:
-                keep_y(i - 2)
-
-            if is_step(i + 1):
-                for w in (SIGMA, MU, ALPHA):
-                    product(w, i + 1)
-
-            if is_block(i - LAG_T):
-                minimum(0, i - LAG_T)
-            if is_block(i - LAG_A):
-                minimum(1, i - LAG_A)
-            if i % 4 == 2 and D <= (i + 2) // 4 < N_CHUNKS * D:
-                quantise_x((i + 2) // 4)
-            if is_step(i):
                 exp_minus_log_sigma(i)
             if is_block(i - LAG_T - 1):
                 sum_of_exp(0, i - LAG_T - 1)
             if is_block(i - LAG_A - 1):
                 sum_of_exp(1, i - LAG_A - 1)
-
-            if i + 2 < KT:
+            if is_block(i - LAG_T):
+                turn_t(i - LAG_T)
+            if is_block(i - LAG_A):
+                turn_a(i - LAG_A)
+            if 6 <= i + 2 < halves:
+                group_weight(SCALAR, SIGMA, *weight_half(i + 2))
+                transpose_weight(ALPHA, *weight_half(i + 2))
+            if i < STEPS - 1:
+                clip_log_sigma(i)
+            mu_minus_y(i)
+            make_neg_a(i)
+            if i < STEPS - 1:
+                exp_minus_log_sigma(i)
+            if i + 1 < halves:
+                quantise_half(i + 1)
+            if i == 3:
+                quantise_x(1)
+            if i % 4 == 2 and 3 <= (i + 2) // 4 < N_CHUNKS * D:
+                quantise_x((i + 2) // 4)
+            if i == 0:
                 for w in (SIGMA, MU, ALPHA):
-                    transpose_weight(w, i + 2)
-            if i % 2 == 1 and X_BANKS <= (i + 5) // 2 < n_x_banks:
-                transpose_x_bank((i + 5) // 2)
-            if 1 <= i - 1 < N_CHUNKS:
-                spread_y(i - 1)
+                    order_weight(w, KT - 1)
+            if is_step(i - 1):
+                square(i - 1)
+            if i < STEPS - 1:
+                divide_by_sigma(i)
 
-        log_sum = const.tile([P, 2, D, n_blocks], F32)
+            if i + 2 < halves:
+                for w in (SIGMA, MU, ALPHA)[1 if i + 2 >= 6 else 0 :]:
+                    group_weight(SCALAR, w, *weight_half(i + 2))
+            if i == 2:
+                spread_sigma_bias()
+            if i == 1:
+                group_tile((0, 1))
+            if i in (1, 2):
+                for j in (2 * i - 2, 2 * i - 1):
+                    group_x0(VECTOR, j, 1)
+            for n in x_bank_at.get(i - 1, ()):
+                empty_x_bank(n)
+            if i == 7:
+                quantise_x(2)
+            if i % 4 == 3 and (i + 1) // 4 < N_CHUNKS * D:
+                keep_y((i + 1) // (D * KT), ((i + 1) // KT) % D)
+
+            if is_step(i + 1):
+                for w in (SIGMA, MU, ALPHA):
+                    product(w, i + 1)
+            if is_block(i + 1 - LAG_T):
+                open_t(i + 1 - LAG_T)
+
+            if is_block(i - LAG_T):
+                minimum(0, i - LAG_T)
+            if is_block(i - LAG_A):
+                minimum(1, i - LAG_A)
+
+            if i + 3 < halves:
+                kt, d = weight_half(i + 3)
+                transpose_weight(SIGMA, kt, d)
+                transpose_weight(MU, kt, d)
+                if i + 3 < 6:
+                    transpose_weight(ALPHA, kt, d)
+            if i in (0, 1):
+                for j in (2 * i, 2 * i + 1):
+                    x_banks[(j, 1)] = transpose_words(x_words[j], turn_psum, "turn")
+            for n in x_bank_at.get(i, ()):
+                transpose_x_bank(n)
+            if i % 4 == 2 and (i + 2) // 4 < N_CHUNKS * D:
+                spread_y((i + 2) // (D * KT), ((i + 2) // KT) % D)
+
+        end = STEPS
+        sum_of_exp(0, end - 6)
+        sum_of_exp(1, end - 5)
+        turn_t(end - 5)
+        for n in range(3):
+            turn_a(end - 4 + n, bank=n)
+        minimum(0, end - 5)
+        sum_of_exp(0, end - 5)
+        minimum(1, end - 4)
+        sum_of_exp(1, end - 4)
+        divide_by_sigma(end - 1)
+        minimum(1, end - 3)
+        sum_of_exp(1, end - 3)
+        square(end - 1)
+        minimum(1, end - 2)
+        sum_of_exp(1, end - 2)
+        for n in range(4):
+            block = end - 4 + n
+            open_t(block)
+            add_turned(block, (neg_a, clipped, half_z2), range(KT - 1), last=False)
+            if n == 1:
+                turn_a(end - 1, bank=0)
+                minimum(1, end - 1)
+                sum_of_exp(1, end - 1)
+        for block in range(end - 4, end):
+            add_turned(block, (neg_a, clipped, half_z2), (KT - 1,), last=True)
+            minimum(0, block)
+            sum_of_exp(0, block)
+
+        log_sum = const.tile([P, 2, D, N_BLOCKS], F32)
         nc.scalar.activation(out=log_sum[:], in_=exp_sum[:], func=ACT.Ln)
-        lse = const.tile([P, 2, D, n_blocks], F32)
+        lse = const.tile([P, 2, D, N_BLOCKS], F32)
         nc.vector.tensor_tensor(out=lse[:], in0=log_sum[:], in1=low[:], op=ALU.subtract)
-        per_d = const.tile([P, D, n_blocks], F32)
+        per_d = const.tile([P, D, N_BLOCKS], F32)
         nc.vector.tensor_tensor(out=per_d[:], in0=lse[:, 0], in1=lse[:, 1], op=ALU.subtract)
+        result = const.tile([P, N_BLOCKS], F32)
         nc.vector.scalar_tensor_tensor(
-            out=result[:, 0:n_blocks],
+            out=result[:],
             in0=per_d[:, 0, :],
             scalar=-math.log(2.0 * math.pi),
             in1=per_d[:, 1, :],
             op0=ALU.add,
             op1=ALU.add,
         )
-        result_bank = tp_psum.tile([P, P], F32, name="result_bank", tag="bank")
-        nc.tensor.transpose(out=result_bank[:], in_=result[:], identity=ident_f32[:])
-        out_rows = const.tile([n_blocks, P], F32)
-        nc.scalar.copy(out=out_rows[:], in_=result_bank[0:n_blocks, :])
-        nc.sync.dma_start(out=out.rearrange("(j p) -> j p", p=P), in_=out_rows[:])
+        nc.sync.dma_start(out=out.rearrange("(p j) -> p j", j=N_BLOCKS), in_=result[:])

@@ -31,8 +31,10 @@ LAG_A = 4
 VECTOR_A = (1, 3)
 CLIP = 20.0
 SIGMA, MU, ALPHA = 0, 1, 2
+WHOLE_PAIRS = 3
 VECTOR, SCALAR = 0, 1
-X_ENGINE = SCALAR
+X_ENGINE = (SCALAR, VECTOR)
+W_ENGINES = (SCALAR, SCALAR, SCALAR)
 N_BLOCKS = B // P
 
 FLOPS = 2 * B * K * H * D * 3
@@ -48,33 +50,52 @@ def tile_rnadeoutputlayer_t_kernel(
     with ExitStack() as ctx:
         const = ctx.enter_context(tc.tile_pool(name="const", bufs=1))
         raw = ctx.enter_context(tc.tile_pool(name="raw", bufs=1))
-        word_pool = ctx.enter_context(tc.tile_pool(name="words", bufs=KT + 3 * KT))
+        word_pool = ctx.enter_context(tc.tile_pool(name="words", bufs=BLOCKS + 2 + 3 * KT))
         stage = ctx.enter_context(tc.tile_pool(name="stage", bufs=3))
         work = ctx.enter_context(tc.tile_pool(name="work", bufs=4))
-        keep = ctx.enter_context(tc.tile_pool(name="keep", bufs=3 * KT))
+        keep = ctx.enter_context(tc.tile_pool(name="keep", bufs=10))
         mx_psum = ctx.enter_context(tc.psum_pool(name="mx_psum", bufs=1))
         turn_psum = ctx.enter_context(tc.psum_pool(name="turn_psum", bufs=3))
         in_psum = ctx.enter_context(tc.psum_pool(name="in_psum", bufs=2))
         ctx.enter_context(tc.manual_schedule())
 
-        x_blocks = x.rearrange("(p j) h d -> j p (h d)", j=N_BLOCKS)
+        x_pairs = x.rearrange("(p u j) h d -> u p (j h d)", u=N_BLOCKS // 2, j=2)
+
+        def load_pair(pair):
+            tile_ = raw.tile([P, 2, H * D], BF16, name="x_pair%d" % pair)
+            nc.sync.dma_start(out=tile_[:].rearrange("p j c -> p (j c)"), in_=x_pairs[pair])
+            return tile_
 
         x_quarters = x.rearrange("b h d -> (b h d)").rearrange(
-            "(q r c m t e) -> c r t q m e",
-            q=ROWS, r=PACK, c=N_CHUNKS, m=BLOCKS * (H // (PACK * RUN)), t=PACK, e=RUN * D,
+            "(q r u m t e) -> u r t q m e",
+            q=ROWS, r=PACK, u=N_BLOCKS // 2, m=2 * (H // (PACK * RUN)), t=PACK, e=RUN * D,
         )
 
-        def load_quarter_rows(chunk):
-            tile_ = raw.tile([P, PACK, BLOCKS, P, D], BF16, name="x_quarters%d" % chunk)
+        def load_quarter_rows(pair):
+            tile_ = raw.tile([P, PACK, 2, P, D], BF16, name="x_quarters%d" % pair)
             for r in range(PACK):
                 for t in range(PACK):
                     nc.sync.dma_start(
                         out=tile_[ROWS * t : ROWS * (t + 1), r].rearrange(
                             "q j (g i) d -> q (j g) (i d)", i=RUN
                         ),
-                        in_=x_quarters[chunk, r, t],
+                        in_=x_quarters[pair, r, t],
                     )
             return tile_
+
+        v_raws = {}
+
+        def load_weights(kt):
+            for w in (SIGMA, MU, ALPHA):
+                v_raws[(w, kt)] = raw.tile([P, H * D], BF16, name="v_raw", bufs=9)
+                nc.sync.dma_start(
+                    out=v_raws[(w, kt)][:],
+                    in_=weights[w][kt * P : (kt + 1) * P].rearrange("k h d -> k (h d)"),
+                )
+
+        x_raws = {}
+        for pair in range(2):
+            x_raws[pair] = load_pair(pair)
 
         small_rows = const.tile([P, P, D], BF16)
         nc.vector.memset(small_rows[:], 0.0)
@@ -88,24 +109,6 @@ def tile_rnadeoutputlayer_t_kernel(
             out=y_cols[:].rearrange("p j d -> p (j d)"),
             in_=input_var.rearrange("(p j) d -> p (j d)", j=N_BLOCKS),
         )
-        sigma_row = const.tile([P, K * D], BF16)
-        nc.gpsimd.memset(sigma_row[:].bitcast(I32), 0)
-        nc.scalar.dma_start(out=sigma_row[0:1, :], in_=b_sigma.rearrange("(o k) d -> o (k d)", o=1))
-
-        x_raws = []
-        for j in range(BLOCKS):
-            x_raws.append(raw.tile([P, H * D], BF16, name="x_raw%d" % j))
-            nc.sync.dma_start(out=x_raws[j][:], in_=x_blocks[j])
-        v_raws = {}
-
-        def load_weights(kt):
-            for w in (SIGMA, MU, ALPHA):
-                v_raws[(w, kt)] = raw.tile([P, H * D], BF16, name="v_raw", bufs=9)
-                nc.sync.dma_start(
-                    out=v_raws[(w, kt)][:],
-                    in_=weights[w][kt * P : (kt + 1) * P].rearrange("k h d -> k (h d)"),
-                )
-
         for kt in range(KT - 1):
             load_weights(kt)
         x_quarter_tiles = {}
@@ -119,9 +122,6 @@ def tile_rnadeoutputlayer_t_kernel(
             out=perm[:].rearrange("p (q t) -> p t q", t=PACK),
             in_=ident_bf16[:].rearrange("p (t q) -> p t q", t=PACK),
         )
-        ones = const.tile([P, P], BF16)
-        nc.vector.memset(ones[:], 1.0)
-
         warm = const.tile([P, 2], F32)
         nc.vector.memset(warm[:], 0.0)
         nc.scalar.activation(out=warm[:, 1:2], in_=warm[:, 0:1], func=ACT.Exp)
@@ -133,7 +133,7 @@ def tile_rnadeoutputlayer_t_kernel(
         exp_bias = const.tile([P, D, KT], F32)
         clip_low = const.tile([P, D, KT], F32)
         clip_high = const.tile([P, D, KT], F32)
-        sigma_bias = const.tile([P, D, K], BF16)
+        b_sig_cols = const.tile([P, D, KT], F32)
         small_bank = {}
 
         def transpose_small():
@@ -157,13 +157,11 @@ def tile_rnadeoutputlayer_t_kernel(
                 op0=ALU.mult, op1=ALU.add,
             )
             nc.vector.tensor_copy(out=b_mu_cols[:], in_=small[:, :, KT * MU : KT * (MU + 1)])
+            nc.vector.tensor_copy(out=b_sig_cols[:], in_=b_sig)
             nc.vector.tensor_scalar(
                 out=neg_b_alp[:], in0=small[:, :, KT * ALPHA : KT * (ALPHA + 1)],
                 scalar1=-1.0, scalar2=None, op0=ALU.mult,
             )
-
-        def spread_sigma_bias():
-            nc.scalar.copy(out=sigma_bias[:], in_=sigma_row[:].rearrange("p (k d) -> p d k", d=D))
 
         y_banks = {}
         y_all = {}
@@ -189,12 +187,8 @@ def tile_rnadeoutputlayer_t_kernel(
         low = const.tile([P, 2, D, N_BLOCKS], F32)
         exp_sum = const.tile([P, 2, D, N_BLOCKS], F32)
 
-        v_codes = [
-            const.tile([P, KT, D, P], U32, name="v_codes%d" % w, align_bytes=64) for w in range(3)
-        ]
-        v_scales = [
-            const.tile([P, KT, D, P], U8, name="v_scales%d" % w, align_bytes=64) for w in range(3)
-        ]
+        v_codes = const.tile([P, KT, D, 3, P], U32, align_bytes=64)
+        v_scales = const.tile([P, KT, D, 3, P], U8, align_bytes=64)
 
         def copy_on(engine, out, in_):
             if engine == 0:
@@ -202,21 +196,18 @@ def tile_rnadeoutputlayer_t_kernel(
             else:
                 nc.scalar.copy(out=out, in_=in_)
 
-        def order_words(raw_tile):
+        def order_words(raw_row):
             words = word_pool.tile([P, PACK, P], F32, name="words")
             nc.vector.tensor_copy(
                 out=words[:].rearrange("p t (g i) -> p t g i", i=RUN),
-                in_=raw_tile[:].bitcast(F32).rearrange("p (g t i) -> p t g i", t=PACK, i=RUN),
+                in_=raw_row.bitcast(F32).rearrange("p (g t i) -> p t g i", t=PACK, i=RUN),
             )
             return words
 
-        def transpose_words(words, pool, tag):
+        def transpose_words(words, d, pool, tag):
             bank = pool.tile([P, PACK, P], F32, name="word_bank", tag=tag)
             for t in range(PACK):
                 nc.tensor.transpose(out=bank[:, t, :], in_=words[:, t, :], identity=ident_f32[:])
-            return bank
-
-        def one_d(bank, d):
             return (
                 bank[:]
                 .rearrange("p t r -> p (t r)")
@@ -229,22 +220,20 @@ def tile_rnadeoutputlayer_t_kernel(
         v_grouped = {}
 
         def order_weight(w, kt):
-            v_words[(w, kt)] = order_words(v_raws[(w, kt)])
+            v_words[(w, kt)] = order_words(v_raws[(w, kt)][:])
 
         def transpose_weight(w, kt, d):
-            if w == ALPHA and d * KT + kt < 6:
-                v_banks[(w, kt, d)] = transpose_words(v_words[(w, kt)], turn_psum, "turn")
-            else:
-                v_banks[(w, kt, d)] = transpose_words(v_words[(w, kt)], in_psum, "in")
+            pool, tag = (turn_psum, "turn") if w == ALPHA and d * KT + kt < 6 else (in_psum, "in")
+            v_banks[(w, kt, d)] = transpose_words(v_words[(w, kt)], d, pool, tag)
 
         def group_weight(engine, w, kt, d):
             v_grouped[(w, kt, d)] = stage.tile([P, P, PACK], BF16, name="v_grouped", align_bytes=64, bufs=6)
-            copy_on(engine, v_grouped[(w, kt, d)][:], one_d(v_banks[(w, kt, d)], d))
+            copy_on(engine, v_grouped[(w, kt, d)][:], v_banks[(w, kt, d)])
 
         def quantise_weight(w, kt, d):
             nc.vector.quantize_mx(
-                out=v_codes[w][:, kt, d].bitcast(FP8X4),
-                scales=v_scales[w][:, kt, d],
+                out=v_codes[:, kt, d, w].bitcast(FP8X4),
+                scales=v_scales[:, kt, d, w],
                 in_=v_grouped[(w, kt, d)][:].rearrange("p k t -> p (k t)"),
             )
 
@@ -262,32 +251,32 @@ def tile_rnadeoutputlayer_t_kernel(
         def x_bank_place(n):
             return n // X_BANKS, (n % X_BANKS) // 2, n % 2
 
-        def transpose_x_bank(n):
+        def transpose_x_bank(n, pool, tag):
             chunk, d, half = x_bank_place(n)
-            half_rows = PACK // 2
-            bank = in_psum.tile([P, BLOCKS, ROWS, half_rows, PACK], BF16, name="x_bank", tag="in")
-            for r in range(half_rows):
-                for j in range(BLOCKS):
+            pair = 2 * chunk + half
+            if pair < WHOLE_PAIRS:
+                x_banks[n] = [transpose_words(x_words[(pair, j)], d, pool, tag) for j in range(2)]
+                return
+            bank = pool.tile([P, 2, P, PACK], BF16, name="x_bank", tag=tag)
+            for j in range(2):
+                for r in range(PACK):
                     nc.tensor.transpose(
-                        out=bank[:, j, :, r, :],
-                        in_=x_quarter_tiles[chunk][:, half * half_rows + r, j, :, d],
+                        out=bank[:, j].rearrange("p (q r) t -> p q r t", r=PACK)[:, :, r, :],
+                        in_=x_quarter_tiles[pair][:, r, j, :, d],
                         identity=perm[:],
                     )
-            x_banks[n] = bank
+            x_banks[n] = [bank[:]]
 
-        def empty_x_bank(n):
+        def empty_x_bank(n, engines):
             chunk, d, half = x_bank_place(n)
             if half == 0:
                 group_tile((chunk, d))
-            half_rows = PACK // 2
-            copy_on(
-                X_ENGINE,
-                x_grouped[(chunk, d)][:]
-                .rearrange("p j (q s) t -> p (j q) (s t)", s=PACK)[
-                    :, :, half * half_rows * PACK : (half + 1) * half_rows * PACK
-                ],
-                x_banks[n][:].rearrange("p j q r t -> p (j q) (r t)"),
-            )
+            grouped = x_grouped[(chunk, d)][:, 2 * half : 2 * half + 2]
+            if len(x_banks[n]) == 2:
+                for j in range(2):
+                    copy_on(engines[j], grouped[:, j], x_banks[n][j])
+            else:
+                copy_on(engines[0], grouped, x_banks[n][0])
 
         def quantise_x(g):
             group = (g // D, g % D)
@@ -316,8 +305,8 @@ def tile_rnadeoutputlayer_t_kernel(
             acc[(w, step)] = mx_psum.tile([P, N_COLS], F32, name="acc%d" % w)
             nc.tensor.matmul_mx(
                 out=acc[(w, step)][:],
-                lhsT=v_codes[w][:, kt, d, :].bitcast(FP8X4),
-                lhsT_scale=v_scales[w][:, kt, d, :],
+                lhsT=v_codes[:, kt, d, w, :].bitcast(FP8X4),
+                lhsT_scale=v_scales[:, kt, d, w, :],
                 rhs=x_codes[(chunk, d)][:].bitcast(FP8X4),
                 rhs_scale=x_scales[(chunk, d)][:],
                 start=True,
@@ -417,32 +406,32 @@ def tile_rnadeoutputlayer_t_kernel(
                     identity=ident_f32[:],
                 )
 
-        def add_turned(block, parts, kts, last):
+        def add_turned(block, kts):
             first_step = (block // BLOCKS) * KT
             j = block % BLOCKS
-            terms = [(part, kt) for part in parts for kt in kts]
-            for n, (part, kt) in enumerate(terms):
-                nc.tensor.matmul(
-                    out=turned[(0, block)][:, kt * P : (kt + 1) * P],
-                    lhsT=part[first_step + kt][:, j * P : (j + 1) * P],
-                    rhs=ident_f32[:],
-                    start=False,
-                    stop=(last and n == len(terms) - 1),
-                    is_transpose=True,
-                )
+            d = (block // BLOCKS) % D
+            for kt in kts:
+                parts = [b_sig_cols[:, d, kt : kt + 1].to_broadcast([P, P])]
+                parts += [part[first_step + kt][:, j * P : (j + 1) * P] for part in (neg_a, clipped, half_z2)]
+                for n, part in enumerate(parts):
+                    nc.tensor.matmul(
+                        out=turned[(0, block)][:, kt * P : (kt + 1) * P],
+                        lhsT=part,
+                        rhs=ident_f32[:],
+                        start=(kt == 0 and n == 0),
+                        stop=(kt == KT - 1 and n == len(parts) - 1),
+                        is_transpose=True,
+                    )
 
         def open_t(block):
-            d = (block // BLOCKS) % D
             if block >= STEPS - 2:
                 turned[(0, block)] = in_psum.tile([P, K], F32, name="turned_t", tag="in")
             else:
                 turned[(0, block)] = turn_psum.tile([P, K], F32, name="turned_t", tag="turn")
-            nc.tensor.matmul(
-                out=turned[(0, block)][:], lhsT=ones[:], rhs=sigma_bias[:, d, :], start=True, stop=False
-            )
 
         def turn_t(block):
-            add_turned(block, (neg_a, clipped, half_z2), range(KT), last=True)
+            open_t(block)
+            add_turned(block, range(KT))
 
         def minimum(kind, block):
             nc.vector.tensor_reduce(
@@ -471,88 +460,70 @@ def tile_rnadeoutputlayer_t_kernel(
         def is_block(block):
             return 0 <= block < STEPS
 
-        def group_x0(engine, j, d):
-            copy_on(engine, x_grouped[(0, d)][:, j], one_d(x_banks[(j, d)], d))
+        halves = D * KT
 
         def weight_half(h):
             return h % KT, h // KT
-
-        def transpose_half(h):
-            for w in (SIGMA, MU, ALPHA):
-                transpose_weight(w, *weight_half(h))
-
-        def group_half(h):
-            for w in (SIGMA, MU, ALPHA):
-                group_weight(SCALAR, w, *weight_half(h))
 
         def quantise_half(h):
             for w in (SIGMA, MU, ALPHA):
                 quantise_weight(w, *weight_half(h))
 
-        halves = D * KT
-
         x_bank_at = {}
-        for g in range(D, N_CHUNKS * D):
+        for g in range(D + 1, N_CHUNKS * D):
             for half in range(2):
-                x_bank_at.setdefault(KT * g - KT - 1 + (2 if g == D else 0) + half, []).append(2 * g + half)
+                x_bank_at.setdefault(KT * g - KT - 1 + half, []).append(2 * g + half)
 
-        for j in range(BLOCKS):
-            x_words[j] = order_words(x_raws[j])
-        group_tile((0, 0))
-        for j in range(BLOCKS):
-            if j < 2:
-                x_banks[(j, 0)] = transpose_words(x_words[j], in_psum, "in")
-            else:
-                x_banks[(j, 0)] = transpose_words(x_words[j], turn_psum, "turn")
+        both = (VECTOR, SCALAR)
+        for pair in range(2):
+            for j in range(2):
+                x_words[(pair, j)] = order_words(x_raws[pair][:, j])
+            transpose_x_bank(pair, *((in_psum, "in") if pair == 0 else (turn_psum, "turn")))
         order_weight(SIGMA, 0)
-        group_x0(VECTOR, 0, 0)
-        group_x0(SCALAR, 1, 0)
-        order_weight(MU, 0)
-        group_x0(VECTOR, 2, 0)
-        group_x0(SCALAR, 3, 0)
-        order_weight(ALPHA, 0)
-        load_weights(KT - 1)
-        for chunk in range(1, N_CHUNKS):
-            x_quarter_tiles[chunk] = load_quarter_rows(chunk)
+        empty_x_bank(0, both)
         transpose_weight(SIGMA, 0, 0)
+        order_weight(MU, 0)
+        empty_x_bank(1, both)
         transpose_weight(MU, 0, 0)
         group_weight(SCALAR, SIGMA, 0, 0)
-        quantise_x(0)
         transpose_small()
+        order_weight(ALPHA, 0)
+        load_weights(KT - 1)
+        x_raws[2] = load_pair(2)
+        for pair in range(WHOLE_PAIRS, N_BLOCKS // 2):
+            x_quarter_tiles[pair] = load_quarter_rows(pair)
+        quantise_x(0)
         spread_y(0, 0)
         group_weight(SCALAR, MU, 0, 0)
-        bias_columns()
         quantise_weight(SIGMA, 0, 0)
-        transpose_weight(ALPHA, 0, 0)
-        keep_y(0, 0)
+        bias_columns()
         product(SIGMA, 0)
         quantise_weight(MU, 0, 0)
+        transpose_weight(ALPHA, 0, 0)
+        keep_y(0, 0)
         product(MU, 0)
         group_weight(SCALAR, ALPHA, 0, 0)
         for w in (SIGMA, MU, ALPHA):
             order_weight(w, 1)
-        transpose_half(1)
+            transpose_weight(w, 1, 0)
         quantise_weight(ALPHA, 0, 0)
         product(ALPHA, 0)
         for w in (SIGMA, MU, ALPHA):
+            group_weight(SCALAR, w, 1, 0)
+        for w in (SIGMA, MU, ALPHA):
             order_weight(w, 2)
-        group_half(1)
-        transpose_half(2)
+            transpose_weight(w, 2, 0)
 
         for i in range(STEPS):
+            if is_block(i - LAG_T - 1):
+                sum_of_exp(0, i - LAG_T - 1)
             if i == STEPS - 1:
                 clip_log_sigma(i)
                 exp_minus_log_sigma(i)
-            if is_block(i - LAG_T - 1):
-                sum_of_exp(0, i - LAG_T - 1)
             if is_block(i - LAG_A - 1):
                 sum_of_exp(1, i - LAG_A - 1)
-            if is_block(i - LAG_T):
-                turn_t(i - LAG_T)
-            if is_block(i - LAG_A):
-                turn_a(i - LAG_A)
             if 6 <= i + 2 < halves:
-                group_weight(SCALAR, SIGMA, *weight_half(i + 2))
+                group_weight(W_ENGINES[SIGMA], SIGMA, *weight_half(i + 2))
                 transpose_weight(ALPHA, *weight_half(i + 2))
             if i < STEPS - 1:
                 clip_log_sigma(i)
@@ -560,15 +531,26 @@ def tile_rnadeoutputlayer_t_kernel(
             make_neg_a(i)
             if i < STEPS - 1:
                 exp_minus_log_sigma(i)
+            if i == 4:
+                empty_x_bank(4, both)
+            if i == 5:
+                empty_x_bank(5, both)
+            if is_block(i - LAG_T):
+                turn_t(i - LAG_T)
+            if is_block(i - LAG_A):
+                turn_a(i - LAG_A)
             if i + 1 < halves:
                 quantise_half(i + 1)
             if i == 3:
                 quantise_x(1)
-            if i % 4 == 2 and 3 <= (i + 2) // 4 < N_CHUNKS * D:
+            if i % 4 == 2 and 2 <= (i + 2) // 4 < N_CHUNKS * D:
                 quantise_x((i + 2) // 4)
             if i == 0:
                 for w in (SIGMA, MU, ALPHA):
                     order_weight(w, KT - 1)
+            if i == 1:
+                for j in range(2):
+                    x_words[(2, j)] = order_words(x_raws[2][:, j])
             if is_step(i - 1):
                 square(i - 1)
             if i < STEPS - 1:
@@ -576,26 +558,17 @@ def tile_rnadeoutputlayer_t_kernel(
 
             if i + 2 < halves:
                 for w in (SIGMA, MU, ALPHA)[1 if i + 2 >= 6 else 0 :]:
-                    group_weight(SCALAR, w, *weight_half(i + 2))
-            if i == 2:
-                spread_sigma_bias()
-            if i == 1:
-                group_tile((0, 1))
+                    group_weight(W_ENGINES[w], w, *weight_half(i + 2))
             if i in (1, 2):
-                for j in (2 * i - 2, 2 * i - 1):
-                    group_x0(VECTOR, j, 1)
+                empty_x_bank(D + i - 1, both)
             for n in x_bank_at.get(i - 1, ()):
-                empty_x_bank(n)
-            if i == 7:
-                quantise_x(2)
+                empty_x_bank(n, X_ENGINE)
             if i % 4 == 3 and (i + 1) // 4 < N_CHUNKS * D:
                 keep_y((i + 1) // (D * KT), ((i + 1) // KT) % D)
 
             if is_step(i + 1):
                 for w in (SIGMA, MU, ALPHA):
                     product(w, i + 1)
-            if is_block(i + 1 - LAG_T):
-                open_t(i + 1 - LAG_T)
 
             if is_block(i - LAG_T):
                 minimum(0, i - LAG_T)
@@ -603,27 +576,22 @@ def tile_rnadeoutputlayer_t_kernel(
                 minimum(1, i - LAG_A)
 
             if i + 3 < halves:
-                kt, d = weight_half(i + 3)
-                transpose_weight(SIGMA, kt, d)
-                transpose_weight(MU, kt, d)
-                if i + 3 < 6:
-                    transpose_weight(ALPHA, kt, d)
+                for w in (SIGMA, MU) if i + 3 >= 6 else (SIGMA, MU, ALPHA):
+                    transpose_weight(w, *weight_half(i + 3))
             if i in (0, 1):
-                for j in (2 * i, 2 * i + 1):
-                    x_banks[(j, 1)] = transpose_words(x_words[j], turn_psum, "turn")
+                transpose_x_bank(D + i, turn_psum, "turn")
+            if i in (3, 4):
+                transpose_x_bank(i + 1, turn_psum, "turn")
             for n in x_bank_at.get(i, ()):
-                transpose_x_bank(n)
+                transpose_x_bank(n, in_psum, "in")
             if i % 4 == 2 and (i + 2) // 4 < N_CHUNKS * D:
                 spread_y((i + 2) // (D * KT), ((i + 2) // KT) % D)
 
         end = STEPS
         sum_of_exp(0, end - 6)
         sum_of_exp(1, end - 5)
-        turn_t(end - 5)
         for n in range(3):
             turn_a(end - 4 + n, bank=n)
-        minimum(0, end - 5)
-        sum_of_exp(0, end - 5)
         minimum(1, end - 4)
         sum_of_exp(1, end - 4)
         divide_by_sigma(end - 1)
@@ -632,16 +600,15 @@ def tile_rnadeoutputlayer_t_kernel(
         square(end - 1)
         minimum(1, end - 2)
         sum_of_exp(1, end - 2)
-        for n in range(4):
-            block = end - 4 + n
-            open_t(block)
-            add_turned(block, (neg_a, clipped, half_z2), range(KT - 1), last=False)
-            if n == 1:
+        turn_t(end - 5)
+        minimum(0, end - 5)
+        sum_of_exp(0, end - 5)
+        for block in range(end - 4, end):
+            turn_t(block)
+            if block == end - 4:
                 turn_a(end - 1, bank=0)
                 minimum(1, end - 1)
                 sum_of_exp(1, end - 1)
-        for block in range(end - 4, end):
-            add_turned(block, (neg_a, clipped, half_z2), (KT - 1,), last=True)
             minimum(0, block)
             sum_of_exp(0, block)
 

@@ -109,8 +109,11 @@ def tile_rnadeoutputlayer_t_kernel(
             out=y_cols[:].rearrange("p j d -> p (j d)"),
             in_=input_var.rearrange("(p j) d -> p (j d)", j=N_BLOCKS),
         )
+        sigma_row = const.tile([P, K * D], BF16)
+        nc.gpsimd.memset(sigma_row[:].bitcast(I32), 0)
         for kt in range(KT - 1):
             load_weights(kt)
+        nc.sync.dma_start(out=sigma_row[0:1, :], in_=b_sigma.rearrange("(o k) d -> o (k d)", o=1))
         x_quarter_tiles = {}
 
         ident_bf16 = const.tile([P, P], BF16)
@@ -122,6 +125,9 @@ def tile_rnadeoutputlayer_t_kernel(
             out=perm[:].rearrange("p (q t) -> p t q", t=PACK),
             in_=ident_bf16[:].rearrange("p (t q) -> p t q", t=PACK),
         )
+        ones = const.tile([P, P], BF16)
+        nc.vector.memset(ones[:], 1.0)
+
         warm = const.tile([P, 2], F32)
         nc.vector.memset(warm[:], 0.0)
         nc.scalar.activation(out=warm[:, 1:2], in_=warm[:, 0:1], func=ACT.Exp)
@@ -133,7 +139,7 @@ def tile_rnadeoutputlayer_t_kernel(
         exp_bias = const.tile([P, D, KT], F32)
         clip_low = const.tile([P, D, KT], F32)
         clip_high = const.tile([P, D, KT], F32)
-        b_sig_cols = const.tile([P, D, KT], F32)
+        sigma_bias = const.tile([P, D, K], BF16)
         small_bank = {}
 
         def transpose_small():
@@ -157,11 +163,13 @@ def tile_rnadeoutputlayer_t_kernel(
                 op0=ALU.mult, op1=ALU.add,
             )
             nc.vector.tensor_copy(out=b_mu_cols[:], in_=small[:, :, KT * MU : KT * (MU + 1)])
-            nc.vector.tensor_copy(out=b_sig_cols[:], in_=b_sig)
             nc.vector.tensor_scalar(
                 out=neg_b_alp[:], in0=small[:, :, KT * ALPHA : KT * (ALPHA + 1)],
                 scalar1=-1.0, scalar2=None, op0=ALU.mult,
             )
+
+        def spread_sigma_bias():
+            nc.scalar.copy(out=sigma_bias[:], in_=sigma_row[:].rearrange("p (k d) -> p d k", d=D))
 
         y_banks = {}
         y_all = {}
@@ -406,32 +414,30 @@ def tile_rnadeoutputlayer_t_kernel(
                     identity=ident_f32[:],
                 )
 
-        def add_turned(block, kts):
-            first_step = (block // BLOCKS) * KT
-            j = block % BLOCKS
-            d = (block // BLOCKS) % D
-            for kt in kts:
-                parts = [b_sig_cols[:, d, kt : kt + 1].to_broadcast([P, P])]
-                parts += [part[first_step + kt][:, j * P : (j + 1) * P] for part in (neg_a, clipped, half_z2)]
-                for n, part in enumerate(parts):
-                    nc.tensor.matmul(
-                        out=turned[(0, block)][:, kt * P : (kt + 1) * P],
-                        lhsT=part,
-                        rhs=ident_f32[:],
-                        start=(kt == 0 and n == 0),
-                        stop=(kt == KT - 1 and n == len(parts) - 1),
-                        is_transpose=True,
-                    )
-
         def open_t(block):
-            if block >= STEPS - 2:
-                turned[(0, block)] = in_psum.tile([P, K], F32, name="turned_t", tag="in")
-            else:
-                turned[(0, block)] = turn_psum.tile([P, K], F32, name="turned_t", tag="turn")
+            pool, tag = (in_psum, "in") if block >= STEPS - 2 else (turn_psum, "turn")
+            turned[(0, block)] = pool.tile([P, K], F32, name="turned_t", tag=tag)
+            nc.tensor.matmul(
+                out=turned[(0, block)][:],
+                lhsT=ones[:],
+                rhs=sigma_bias[:, (block // BLOCKS) % D, :],
+                start=True,
+                stop=False,
+            )
 
         def turn_t(block):
-            open_t(block)
-            add_turned(block, range(KT))
+            first_step = (block // BLOCKS) * KT
+            j = block % BLOCKS
+            terms = [(part, kt) for part in (neg_a, clipped, half_z2) for kt in range(KT)]
+            for n, (part, kt) in enumerate(terms):
+                nc.tensor.matmul(
+                    out=turned[(0, block)][:, kt * P : (kt + 1) * P],
+                    lhsT=part[first_step + kt][:, j * P : (j + 1) * P],
+                    rhs=ident_f32[:],
+                    start=False,
+                    stop=(n == len(terms) - 1),
+                    is_transpose=True,
+                )
 
         def minimum(kind, block):
             nc.vector.tensor_reduce(
@@ -535,6 +541,8 @@ def tile_rnadeoutputlayer_t_kernel(
                 empty_x_bank(4, both)
             if i == 5:
                 empty_x_bank(5, both)
+            if 0 <= i - LAG_T < 2:
+                open_t(i - LAG_T)
             if is_block(i - LAG_T):
                 turn_t(i - LAG_T)
             if is_block(i - LAG_A):
@@ -548,6 +556,8 @@ def tile_rnadeoutputlayer_t_kernel(
             if i == 0:
                 for w in (SIGMA, MU, ALPHA):
                     order_weight(w, KT - 1)
+            if i == 2:
+                spread_sigma_bias()
             if i == 1:
                 for j in range(2):
                     x_words[(2, j)] = order_words(x_raws[2][:, j])
@@ -569,6 +579,8 @@ def tile_rnadeoutputlayer_t_kernel(
             if is_step(i + 1):
                 for w in (SIGMA, MU, ALPHA):
                     product(w, i + 1)
+            if 2 <= i + 1 - LAG_T < STEPS:
+                open_t(i + 1 - LAG_T)
 
             if is_block(i - LAG_T):
                 minimum(0, i - LAG_T)
@@ -604,6 +616,7 @@ def tile_rnadeoutputlayer_t_kernel(
         minimum(0, end - 5)
         sum_of_exp(0, end - 5)
         for block in range(end - 4, end):
+            open_t(block)
             turn_t(block)
             if block == end - 4:
                 turn_a(end - 1, bank=0)
@@ -612,19 +625,25 @@ def tile_rnadeoutputlayer_t_kernel(
             minimum(0, block)
             sum_of_exp(0, block)
 
-        log_sum = const.tile([P, 2, D, N_BLOCKS], F32)
-        nc.scalar.activation(out=log_sum[:], in_=exp_sum[:], func=ACT.Ln)
-        lse = const.tile([P, 2, D, N_BLOCKS], F32)
-        nc.vector.tensor_tensor(out=lse[:], in0=log_sum[:], in1=low[:], op=ALU.subtract)
+        offset = const.tile([P, N_BLOCKS], F32)
         per_d = const.tile([P, D, N_BLOCKS], F32)
-        nc.vector.tensor_tensor(out=per_d[:], in0=lse[:, 0], in1=lse[:, 1], op=ALU.subtract)
-        result = const.tile([P, N_BLOCKS], F32)
+        nc.vector.tensor_tensor(out=per_d[:], in0=low[:, 1], in1=low[:, 0], op=ALU.subtract)
         nc.vector.scalar_tensor_tensor(
-            out=result[:],
+            out=offset[:],
             in0=per_d[:, 0, :],
             scalar=-math.log(2.0 * math.pi),
             in1=per_d[:, 1, :],
             op0=ALU.add,
             op1=ALU.add,
         )
+        product_a = const.tile([P, N_BLOCKS], F32)
+        nc.vector.tensor_tensor(out=product_a[:], in0=exp_sum[:, 1, 0], in1=exp_sum[:, 1, 1], op=ALU.mult)
+        ratio = const.tile([P, N_BLOCKS], F32)
+        nc.vector.reciprocal(out=ratio[:], in_=product_a[:])
+        nc.vector.tensor_tensor(out=ratio[:], in0=ratio[:], in1=exp_sum[:, 0, 0], op=ALU.mult)
+        nc.vector.tensor_tensor(out=ratio[:], in0=ratio[:], in1=exp_sum[:, 0, 1], op=ALU.mult)
+        log_ratio = const.tile([P, N_BLOCKS], F32)
+        nc.scalar.activation(out=log_ratio[:], in_=ratio[:], func=ACT.Ln)
+        result = const.tile([P, N_BLOCKS], F32)
+        nc.vector.tensor_tensor(out=result[:], in0=log_ratio[:], in1=offset[:], op=ALU.add)
         nc.sync.dma_start(out=out.rearrange("(p j) -> p j", j=N_BLOCKS), in_=result[:])

@@ -28,6 +28,7 @@ X_BANKS = 2 * D
 ROWS = P // PACK
 LAG_T = 5
 LAG_A = 4
+SCALAR_SQUARES = (1,)
 VECTOR_A = (1, 3)
 CLIP = 20.0
 SIGMA, MU, ALPHA = 0, 1, 2
@@ -365,7 +366,9 @@ def tile_rnadeoutputlayer_t_kernel(
 
         def square(step):
             half_z2[step] = keep.tile([P, N_COLS], F32, name="half_z2")
-            if step == STEPS - 1:
+            if step % KT in SCALAR_SQUARES and step < STEPS - 1:
+                nc.scalar.activation(out=half_z2[step][:], in_=z[step][:], func=ACT.Square)
+            elif step == STEPS - 1:
                 nc.vector.tensor_tensor(
                     out=half_z2[step][:], in0=z[step][:], in1=z[step][:], op=ALU.mult
                 )

@@ -28,8 +28,8 @@ X_BANKS = 2 * D
 ROWS = P // PACK
 LAG_T = 5
 LAG_A = 4
-SCALAR_SQUARES = (1,)
-VECTOR_A = (1, 3)
+SCALAR_SQUARES = (2,)
+VECTOR_A = (0, 1, 3)
 CLIP = 20.0
 SIGMA, MU, ALPHA = 0, 1, 2
 WHOLE_PAIRS = 3

import math
from contextlib import ExitStack

import concourse.mybir as mybir
from concourse.masks import make_identity

F32 = mybir.dt.float32
BF16 = mybir.dt.bfloat16
U32 = mybir.dt.uint32
I32 = mybir.dt.int32
U8 = mybir.dt.uint8
FP8X4 = mybir.dt.float8_e4m3fn_x4
ALU = mybir.AluOpType
ACT = mybir.ActivationFunctionType
AXIS = mybir.AxisListType

P = 128
PACK = 4
RUN = 8
B, K, H, D = 2048, 512, 512, 2
N_COLS = 512
BANK_BF16 = 1024
KT = K // P
N_CHUNKS = B // N_COLS
BLOCKS = N_COLS // P
STEPS = N_CHUNKS * D * KT
X_BANKS = 2 * D
ROWS = P // PACK
LAG_T = 5
LAG_A = 4
SCALAR_SQUARES = (2,)
VECTOR_A = (0, 1, 3)
CLIP = 20.0
SIGMA, MU, ALPHA = 0, 1, 2
WHOLE_PAIRS = 3
VECTOR, SCALAR = 0, 1
X_ENGINE = (SCALAR, VECTOR)
W_ENGINES = (SCALAR, SCALAR, SCALAR)
N_BLOCKS = B // P

FLOPS = 2 * B * K * H * D * 3


def tile_rnadeoutputlayer_t_kernel(
    tc, x, input_var, V_alpha, V_mu, V_sigma, b_alpha, b_mu, b_sigma, out
):
    nc = tc.nc
    weights = (V_sigma, V_mu, V_alpha)
    biases = (b_sigma, b_mu, b_alpha)

    with ExitStack() as ctx:
        const = ctx.enter_context(tc.tile_pool(name="const", bufs=1))
        raw = ctx.enter_context(tc.tile_pool(name="raw", bufs=1))
        word_pool = ctx.enter_context(tc.tile_pool(name="words", bufs=BLOCKS + 2 + 3 * KT))
        stage = ctx.enter_context(tc.tile_pool(name="stage", bufs=3))
        work = ctx.enter_context(tc.tile_pool(name="work", bufs=4))
        keep = ctx.enter_context(tc.tile_pool(name="keep", bufs=10))
        mx_psum = ctx.enter_context(tc.psum_pool(name="mx_psum", bufs=1))
        turn_psum = ctx.enter_context(tc.psum_pool(name="turn_psum", bufs=3))
        in_psum = ctx.enter_context(tc.psum_pool(name="in_psum", bufs=2))
        ctx.enter_context(tc.manual_schedule())

        x_pairs = x.rearrange("(p u j) h d -> u p (j h d)", u=N_BLOCKS // 2, j=2)

        def load_pair(pair):
            tile_ = raw.tile([P, 2, H * D], BF16, name="x_pair%d" % pair)
            nc.sync.dma_start(out=tile_[:].rearrange("p j c -> p (j c)"), in_=x_pairs[pair])
            return tile_

        x_quarters = x.rearrange("b h d -> (b h d)").rearrange(
            "(q r u m t e) -> u r t q m e",
            q=ROWS, r=PACK, u=N_BLOCKS // 2, m=2 * (H // (PACK * RUN)), t=PACK, e=RUN * D,
        )

        def load_quarter_rows(pair):
            tile_ = raw.tile([P, PACK, 2, P, D], BF16, name="x_quarters%d" % pair)
            for r in range(PACK):
                for t in range(PACK):
                    nc.sync.dma_start(
                        out=tile_[ROWS * t : ROWS * (t + 1), r].rearrange(
                            "q j (g i) d -> q (j g) (i d)", i=RUN
                        ),
                        in_=x_quarters[pair, r, t],
                    )
            return tile_

        v_raws = {}

        def load_weights(kt):
            for w in (SIGMA, MU, ALPHA):
                v_raws[(w, kt)] = raw.tile([P, H * D], BF16, name="v_raw", bufs=9)
                nc.sync.dma_start(
                    out=v_raws[(w, kt)][:],
                    in_=weights[w][kt * P : (kt + 1) * P].rearrange("k h d -> k (h d)"),
                )

        x_raws = {}
        for pair in range(2):
            x_raws[pair] = load_pair(pair)

        small_rows = const.tile([P, P, D], BF16)
        nc.vector.memset(small_rows[:], 0.0)
        for w in (SIGMA, MU, ALPHA):
            nc.scalar.dma_start(
                out=small_rows[KT * w : KT * (w + 1)].rearrange("kt kl d -> kt (kl d)"),
                in_=biases[w].rearrange("(kt kl) d -> kt (kl d)", kt=KT),
            )
        y_cols = const.tile([P, N_BLOCKS, D], BF16)
        nc.scalar.dma_start(
            out=y_cols[:].rearrange("p j d -> p (j d)"),
            in_=input_var.rearrange("(p j) d -> p (j d)", j=N_BLOCKS),
        )
        sigma_row = const.tile([P, K * D], BF16)
        nc.gpsimd.memset(sigma_row[:].bitcast(I32), 0)
        for kt in range(KT - 1):
            load_weights(kt)
        nc.sync.dma_start(out=sigma_row[0:1, :], in_=b_sigma.rearrange("(o k) d -> o (k d)", o=1))
        x_quarter_tiles = {}

        ident_bf16 = const.tile([P, P], BF16)
        make_identity(nc, ident_bf16[:])
        ident_f32 = const.tile([P, P], F32)
        make_identity(nc, ident_f32[:])
        perm = const.tile([P, P], BF16)
        nc.vector.tensor_copy(
            out=perm[:].rearrange("p (q t) -> p t q", t=PACK),
            in_=ident_bf16[:].rearrange("p (t q) -> p t q", t=PACK),
        )
        ones = const.tile([P, P], BF16)
        nc.vector.memset(ones[:], 1.0)

        warm = const.tile([P, 2], F32)
        nc.vector.memset(warm[:], 0.0)
        nc.scalar.activation(out=warm[:, 1:2], in_=warm[:, 0:1], func=ACT.Exp)

        n_small = 3 * KT
        small = const.tile([P, D, n_small], BF16)
        b_mu_cols = const.tile([P, D, KT], F32)
        neg_b_alp = const.tile([P, D, KT], F32)
        exp_bias = const.tile([P, D, KT], F32)
        clip_low = const.tile([P, D, KT], F32)
        clip_high = const.tile([P, D, KT], F32)
        sigma_bias = const.tile([P, D, K], BF16)
        small_bank = {}

        def transpose_small():
            small_bank[0] = turn_psum.tile([P, D, P], BF16, name="small_bank", tag="turn")
            for d in range(D):
                nc.tensor.transpose(
                    out=small_bank[0][:, d, :], in_=small_rows[:, :, d], identity=ident_bf16[:]
                )

        def bias_columns():
            nc.vector.tensor_copy(out=small[:], in_=small_bank[0][:, :, 0:n_small])
            b_sig = small[:, :, KT * SIGMA : KT * (SIGMA + 1)]
            nc.vector.tensor_scalar(
                out=clip_low[:], in0=b_sig, scalar1=-1.0, scalar2=-CLIP, op0=ALU.mult, op1=ALU.add
            )
            nc.vector.tensor_scalar(
                out=clip_high[:], in0=b_sig, scalar1=-1.0, scalar2=CLIP, op0=ALU.mult, op1=ALU.add
            )
            nc.vector.tensor_scalar(
                out=exp_bias[:], in0=b_sig, scalar1=-1.0, scalar2=-0.5 * math.log(2.0),
                op0=ALU.mult, op1=ALU.add,
            )
            nc.vector.tensor_copy(out=b_mu_cols[:], in_=small[:, :, KT * MU : KT * (MU + 1)])
            nc.vector.tensor_scalar(
                out=neg_b_alp[:], in0=small[:, :, KT * ALPHA : KT * (ALPHA + 1)],
                scalar1=-1.0, scalar2=None, op0=ALU.mult,
            )

        def spread_sigma_bias():
            nc.scalar.copy(out=sigma_bias[:], in_=sigma_row[:].rearrange("p (k d) -> p d k", d=D))

        y_banks = {}
        y_all = {}

        def spread_y(chunk, d):
            if chunk == 0:
                y_banks[(chunk, d)] = turn_psum.tile([P, BLOCKS, P], BF16, name="y_bank", tag="turn")
            else:
                y_banks[(chunk, d)] = in_psum.tile([P, BLOCKS, P], BF16, name="y_bank", tag="in")
            for j in range(BLOCKS):
                nc.tensor.transpose(
                    out=y_banks[(chunk, d)][:, j, :],
                    in_=y_cols[:, chunk * BLOCKS + j, d : d + 1].to_broadcast([P, P]),
                    identity=ident_bf16[:],
                )

        def keep_y(chunk, d):
            y_all[(chunk, d)] = const.tile([P, N_COLS], BF16, name="y_all%d_%d" % (chunk, d))
            nc.vector.tensor_copy(
                out=y_all[(chunk, d)][:], in_=y_banks[(chunk, d)][:].rearrange("p j b -> p (j b)")
            )

        low = const.tile([P, 2, D, N_BLOCKS], F32)
        exp_sum = const.tile([P, 2, D, N_BLOCKS], F32)

        v_codes = const.tile([P, KT, D, 3, P], U32, align_bytes=64)
        v_scales = const.tile([P, KT, D, 3, P], U8, align_bytes=64)

        def copy_on(engine, out, in_):
            if engine == 0:
                nc.vector.tensor_copy(out=out, in_=in_)
            else:
                nc.scalar.copy(out=out, in_=in_)

        def order_words(raw_row):
            words = word_pool.tile([P, PACK, P], F32, name="words")
            nc.vector.tensor_copy(
                out=words[:].rearrange("p t (g i) -> p t g i", i=RUN),
                in_=raw_row.bitcast(F32).rearrange("p (g t i) -> p t g i", t=PACK, i=RUN),
            )
            return words

        def transpose_words(words, d, pool, tag):
            bank = pool.tile([P, PACK, P], F32, name="word_bank", tag=tag)
            for t in range(PACK):
                nc.tensor.transpose(out=bank[:, t, :], in_=words[:, t, :], identity=ident_f32[:])
            return (
                bank[:]
                .rearrange("p t r -> p (t r)")
                .bitcast(BF16)
                .rearrange("p (t r d) -> p d r t", t=PACK, d=D)[:, d]
            )

        v_words = {}
        v_banks = {}
        v_grouped = {}

        def order_weight(w, kt):
            v_words[(w, kt)] = order_words(v_raws[(w, kt)][:])

        def transpose_weight(w, kt, d):
            pool, tag = (turn_psum, "turn") if w == ALPHA and d * KT + kt < 6 else (in_psum, "in")
            v_banks[(w, kt, d)] = transpose_words(v_words[(w, kt)], d, pool, tag)

        def group_weight(engine, w, kt, d):
            v_grouped[(w, kt, d)] = stage.tile([P, P, PACK], BF16, name="v_grouped", align_bytes=64, bufs=6)
            copy_on(engine, v_grouped[(w, kt, d)][:], v_banks[(w, kt, d)])

        def quantise_weight(w, kt, d):
            nc.vector.quantize_mx(
                out=v_codes[:, kt, d, w].bitcast(FP8X4),
                scales=v_scales[:, kt, d, w],
                in_=v_grouped[(w, kt, d)][:].rearrange("p k t -> p (k t)"),
            )

        x_grouped = {}
        x_codes = {}
        x_scales = {}
        x_words = {}
        x_banks = {}

        def group_tile(group):
            x_grouped[group] = stage.tile(
                [P, BLOCKS, P, PACK], BF16, name="x_grouped", align_bytes=64, bufs=2
            )

        def x_bank_place(n):
            return n // X_BANKS, (n % X_BANKS) // 2, n % 2

        def transpose_x_bank(n, pool, tag):
            chunk, d, half = x_bank_place(n)
            pair = 2 * chunk + half
            if pair < WHOLE_PAIRS:
                x_banks[n] = [transpose_words(x_words[(pair, j)], d, pool, tag) for j in range(2)]
                return
            bank = pool.tile([P, 2, P, PACK], BF16, name="x_bank", tag=tag)
            for j in range(2):
                for r in range(PACK):
                    nc.tensor.transpose(
                        out=bank[:, j].rearrange("p (q r) t -> p q r t", r=PACK)[:, :, r, :],
                        in_=x_quarter_tiles[pair][:, r, j, :, d],
                        identity=perm[:],
                    )
            x_banks[n] = [bank[:]]

        def empty_x_bank(n, engines):
            chunk, d, half = x_bank_place(n)
            if half == 0:
                group_tile((chunk, d))
            grouped = x_grouped[(chunk, d)][:, 2 * half : 2 * half + 2]
            if len(x_banks[n]) == 2:
                for j in range(2):
                    copy_on(engines[j], grouped[:, j], x_banks[n][j])
            else:
                copy_on(engines[0], grouped, x_banks[n][0])

        def quantise_x(g):
            group = (g // D, g % D)
            x_codes[group] = stage.tile([P, N_COLS], U32, name="x_codes", align_bytes=64)
            x_scales[group] = stage.tile([P, N_COLS], U8, name="x_scales", align_bytes=64)
            nc.vector.quantize_mx(
                out=x_codes[group][:].bitcast(FP8X4),
                scales=x_scales[group][:],
                in_=x_grouped[group][:].rearrange("p j b t -> p (j b t)"),
            )

        acc = {}
        clipped = {}
        inv_sigma = {}
        distance = {}
        z = {}
        half_z2 = {}
        neg_a = {}
        turned = {}

        def place(step):
            return step // (D * KT), (step // KT) % D, step % KT

        def product(w, step):
            chunk, d, kt = place(step)
            acc[(w, step)] = mx_psum.tile([P, N_COLS], F32, name="acc%d" % w)
            nc.tensor.matmul_mx(
                out=acc[(w, step)][:],
                lhsT=v_codes[:, kt, d, w, :].bitcast(FP8X4),
                lhsT_scale=v_scales[:, kt, d, w, :],
                rhs=x_codes[(chunk, d)][:].bitcast(FP8X4),
                rhs_scale=x_scales[(chunk, d)][:],
                start=True,
                stop=True,
            )

        def clip_log_sigma(step):
            chunk, d, kt = place(step)
            clipped[step] = keep.tile([P, N_COLS], F32, name="clipped")
            nc.vector.tensor_scalar(
                out=clipped[step][:],
                in0=acc[(SIGMA, step)][:],
                scalar1=clip_low[:, d, kt : kt + 1],
                scalar2=clip_high[:, d, kt : kt + 1],
                op0=ALU.max,
                op1=ALU.min,
            )

        def exp_minus_log_sigma(step):
            chunk, d, kt = place(step)
            inv_sigma[step] = work.tile([P, N_COLS], F32, name="inv_sigma")
            nc.scalar.activation(
                out=inv_sigma[step][:],
                in_=clipped[step][:],
                func=ACT.Exp,
                bias=exp_bias[:, d, kt : kt + 1],
                scale=-1.0,
            )

        def mu_minus_y(step):
            chunk, d, kt = place(step)
            distance[step] = work.tile([P, N_COLS], F32, name="distance")
            nc.vector.scalar_tensor_tensor(
                out=distance[step][:],
                in0=acc[(MU, step)][:],
                scalar=b_mu_cols[:, d, kt : kt + 1],
                in1=y_all[(chunk, d)][:],
                op0=ALU.add,
                op1=ALU.subtract,
            )

        def divide_by_sigma(step):
            z[step] = work.tile([P, N_COLS], F32, name="z")
            engine = nc.vector if step == STEPS - 1 else nc.gpsimd
            engine.tensor_tensor(
                out=z[step][:], in0=distance[step][:], in1=inv_sigma[step][:], op=ALU.mult
            )

        def square(step):
            half_z2[step] = keep.tile([P, N_COLS], F32, name="half_z2")
            if step % KT in SCALAR_SQUARES and step < STEPS - 1:
                nc.scalar.activation(out=half_z2[step][:], in_=z[step][:], func=ACT.Square)
            elif step == STEPS - 1:
                nc.vector.tensor_tensor(
                    out=half_z2[step][:], in0=z[step][:], in1=z[step][:], op=ALU.mult
                )
            else:
                nc.gpsimd.tensor_tensor(
                    out=half_z2[step][:], in0=z[step][:], in1=z[step][:], op=ALU.mult
                )

        def make_neg_a(step):
            chunk, d, kt = place(step)
            neg_a[step] = keep.tile([P, N_COLS], F32, name="neg_a")
            if kt in VECTOR_A:
                nc.vector.tensor_scalar(
                    out=neg_a[step][:],
                    in0=acc[(ALPHA, step)][:],
                    scalar1=-1.0,
                    scalar2=neg_b_alp[:, d, kt : kt + 1],
                    op0=ALU.mult,
                    op1=ALU.add,
                )
                return
            nc.scalar.activation(
                out=neg_a[step][:],
                in_=acc[(ALPHA, step)][:],
                func=ACT.Identity,
                bias=neg_b_alp[:, d, kt : kt + 1],
                scale=-1.0,
            )

        def statistic(tile_, kind, block):
            chunk, d, j = block // (D * BLOCKS), (block // BLOCKS) % D, block % BLOCKS
            column = chunk * BLOCKS + j
            return tile_[:, kind, d, column : column + 1]

        def turn_a(block, bank=None):
            first_step = (block // BLOCKS) * KT
            j = block % BLOCKS
            if bank is None:
                turned[(1, block)] = turn_psum.tile([P, K], F32, name="turned_a", tag="turn")
            else:
                turned[(1, block)] = mx_psum.tile([P, K], F32, name="acc%d" % bank)
            for kt in range(KT):
                nc.tensor.transpose(
                    out=turned[(1, block)][:, kt * P : (kt + 1) * P],
                    in_=neg_a[first_step + kt][:, j * P : (j + 1) * P],
                    identity=ident_f32[:],
                )

        def open_t(block):
            pool, tag = (in_psum, "in") if block >= STEPS - 2 else (turn_psum, "turn")
            turned[(0, block)] = pool.tile([P, K], F32, name="turned_t", tag=tag)
            nc.tensor.matmul(
                out=turned[(0, block)][:],
                lhsT=ones[:],
                rhs=sigma_bias[:, (block // BLOCKS) % D, :],
                start=True,
                stop=False,
            )

        def turn_t(block):
            first_step = (block // BLOCKS) * KT
            j = block % BLOCKS
            terms = [(part, kt) for part in (neg_a, clipped, half_z2) for kt in range(KT)]
            for n, (part, kt) in enumerate(terms):
                nc.tensor.matmul(
                    out=turned[(0, block)][:, kt * P : (kt + 1) * P],
                    lhsT=part[first_step + kt][:, j * P : (j + 1) * P],
                    rhs=ident_f32[:],
                    start=False,
                    stop=(n == len(terms) - 1),
                    is_transpose=True,
                )

        def minimum(kind, block):
            nc.vector.tensor_reduce(
                out=statistic(low, kind, block),
                in_=turned[(kind, block)][:],
                axis=AXIS.X,
                op=ALU.min,
            )

        def sum_of_exp(kind, block):
            unread = work.tile([P, K], F32, name="unread", bufs=2)
            nc.scalar.activation(
                out=unread[:],
                in_=turned[(kind, block)][:],
                func=ACT.Exp,
                bias=statistic(low, kind, block),
                scale=-1.0,
                accum_out=statistic(exp_sum, kind, block),
            )

        n_x_banks = N_CHUNKS * X_BANKS

        def is_step(step):
            return 0 <= step < STEPS

        def is_block(block):
            return 0 <= block < STEPS

        halves = D * KT

        def weight_half(h):
            return h % KT, h // KT

        def quantise_half(h):
            for w in (SIGMA, MU, ALPHA):
                quantise_weight(w, *weight_half(h))

        x_bank_at = {}
        for g in range(D + 1, N_CHUNKS * D):
            for half in range(2):
                x_bank_at.setdefault(KT * g - KT - 1 + half, []).append(2 * g + half)

        both = (VECTOR, SCALAR)
        for pair in range(2):
            for j in range(2):
                x_words[(pair, j)] = order_words(x_raws[pair][:, j])
            transpose_x_bank(pair, *((in_psum, "in") if pair == 0 else (turn_psum, "turn")))
        order_weight(SIGMA, 0)
        empty_x_bank(0, both)
        transpose_weight(SIGMA, 0, 0)
        order_weight(MU, 0)
        empty_x_bank(1, both)
        transpose_weight(MU, 0, 0)
        group_weight(SCALAR, SIGMA, 0, 0)
        transpose_small()
        order_weight(ALPHA, 0)
        load_weights(KT - 1)
        x_raws[2] = load_pair(2)
        for pair in range(WHOLE_PAIRS, N_BLOCKS // 2):
            x_quarter_tiles[pair] = load_quarter_rows(pair)
        quantise_x(0)
        spread_y(0, 0)
        group_weight(SCALAR, MU, 0, 0)
        quantise_weight(SIGMA, 0, 0)
        bias_columns()
        product(SIGMA, 0)
        quantise_weight(MU, 0, 0)
        transpose_weight(ALPHA, 0, 0)
        keep_y(0, 0)
        product(MU, 0)
        group_weight(SCALAR, ALPHA, 0, 0)
        for w in (SIGMA, MU, ALPHA):
            order_weight(w, 1)
            transpose_weight(w, 1, 0)
        quantise_weight(ALPHA, 0, 0)
        product(ALPHA, 0)
        for w in (SIGMA, MU, ALPHA):
            group_weight(SCALAR, w, 1, 0)
        for w in (SIGMA, MU, ALPHA):
            order_weight(w, 2)
            transpose_weight(w, 2, 0)

        for i in range(STEPS):
            if is_block(i - LAG_T - 1):
                sum_of_exp(0, i - LAG_T - 1)
            if i == STEPS - 1:
                clip_log_sigma(i)
                exp_minus_log_sigma(i)
            if is_block(i - LAG_A - 1):
                sum_of_exp(1, i - LAG_A - 1)
            if 6 <= i + 2 < halves:
                group_weight(W_ENGINES[SIGMA], SIGMA, *weight_half(i + 2))
                transpose_weight(ALPHA, *weight_half(i + 2))
            if i < STEPS - 1:
                clip_log_sigma(i)
            mu_minus_y(i)
            make_neg_a(i)
            if i < STEPS - 1:
                exp_minus_log_sigma(i)
            if i == 4:
                empty_x_bank(4, both)
            if i == 5:
                empty_x_bank(5, both)
            if 0 <= i - LAG_T < 2:
                open_t(i - LAG_T)
            if is_block(i - LAG_T):
                turn_t(i - LAG_T)
            if is_block(i - LAG_A):
                turn_a(i - LAG_A)
            if i + 1 < halves:
                quantise_half(i + 1)
            if i == 3:
                quantise_x(1)
            if i % 4 == 2 and 2 <= (i + 2) // 4 < N_CHUNKS * D:
                quantise_x((i + 2) // 4)
            if i == 0:
                for w in (SIGMA, MU, ALPHA):
                    order_weight(w, KT - 1)
            if i == 2:
                spread_sigma_bias()
            if i == 1:
                for j in range(2):
                    x_words[(2, j)] = order_words(x_raws[2][:, j])
            if is_step(i - 1):
                square(i - 1)
            if i < STEPS - 1:
                divide_by_sigma(i)

            if i + 2 < halves:
                for w in (SIGMA, MU, ALPHA)[1 if i + 2 >= 6 else 0 :]:
                    group_weight(W_ENGINES[w], w, *weight_half(i + 2))
            if i in (1, 2):
                empty_x_bank(D + i - 1, both)
            for n in x_bank_at.get(i - 1, ()):
                empty_x_bank(n, X_ENGINE)
            if i % 4 == 3 and (i + 1) // 4 < N_CHUNKS * D:
                keep_y((i + 1) // (D * KT), ((i + 1) // KT) % D)

            if is_step(i + 1):
                for w in (SIGMA, MU, ALPHA):
                    product(w, i + 1)
            if 2 <= i + 1 - LAG_T < STEPS:
                open_t(i + 1 - LAG_T)

            if is_block(i - LAG_T):
                minimum(0, i - LAG_T)
            if is_block(i - LAG_A):
                minimum(1, i - LAG_A)

            if i + 3 < halves:
                for w in (SIGMA, MU) if i + 3 >= 6 else (SIGMA, MU, ALPHA):
                    transpose_weight(w, *weight_half(i + 3))
            if i in (0, 1):
                transpose_x_bank(D + i, turn_psum, "turn")
            if i in (3, 4):
                transpose_x_bank(i + 1, turn_psum, "turn")
            for n in x_bank_at.get(i, ()):
                transpose_x_bank(n, in_psum, "in")
            if i % 4 == 2 and (i + 2) // 4 < N_CHUNKS * D:
                spread_y((i + 2) // (D * KT), ((i + 2) // KT) % D)

        end = STEPS
        sum_of_exp(0, end - 6)
        sum_of_exp(1, end - 5)
        for n in range(3):
            turn_a(end - 4 + n, bank=n)
        minimum(1, end - 4)
        sum_of_exp(1, end - 4)
        divide_by_sigma(end - 1)
        minimum(1, end - 3)
        sum_of_exp(1, end - 3)
        square(end - 1)
        minimum(1, end - 2)
        sum_of_exp(1, end - 2)
        turn_t(end - 5)
        minimum(0, end - 5)
        sum_of_exp(0, end - 5)
        for block in range(end - 4, end):
            open_t(block)
            turn_t(block)
            if block == end - 4:
                turn_a(end - 1, bank=0)
                minimum(1, end - 1)
                sum_of_exp(1, end - 1)
            minimum(0, block)
            sum_of_exp(0, block)

        offset = const.tile([P, N_BLOCKS], F32)
        per_d = const.tile([P, D, N_BLOCKS], F32)
        nc.vector.tensor_tensor(out=per_d[:], in0=low[:, 1], in1=low[:, 0], op=ALU.subtract)
        nc.vector.scalar_tensor_tensor(
            out=offset[:],
            in0=per_d[:, 0, :],
            scalar=-math.log(2.0 * math.pi),
            in1=per_d[:, 1, :],
            op0=ALU.add,
            op1=ALU.add,
        )
        product_a = const.tile([P, N_BLOCKS], F32)
        nc.vector.tensor_tensor(out=product_a[:], in0=exp_sum[:, 1, 0], in1=exp_sum[:, 1, 1], op=ALU.mult)
        ratio = const.tile([P, N_BLOCKS], F32)
        nc.vector.reciprocal(out=ratio[:], in_=product_a[:])
        nc.vector.tensor_tensor(out=ratio[:], in0=ratio[:], in1=exp_sum[:, 0, 0], op=ALU.mult)
        nc.vector.tensor_tensor(out=ratio[:], in0=ratio[:], in1=exp_sum[:, 0, 1], op=ALU.mult)
        log_ratio = const.tile([P, N_BLOCKS], F32)
        nc.scalar.activation(out=log_ratio[:], in_=ratio[:], func=ACT.Ln)
        result = const.tile([P, N_BLOCKS], F32)
        nc.vector.tensor_tensor(out=result[:], in0=log_ratio[:], in1=offset[:], op=ALU.add)
        nc.sync.dma_start(out=out.rearrange("(p j) -> p j", j=N_BLOCKS), in_=result[:])
